import numpy as np
import ml_dtypes


def mxq(x, axis, fmt="e4m3"):
    dtype, down = {"e4m3": (ml_dtypes.float8_e4m3fn, 7), "e5m2": (ml_dtypes.float8_e5m2, 14)}[fmt]
    v = np.moveaxis(np.asarray(x, np.float32).astype(ml_dtypes.bfloat16).astype(np.float64), axis, -1)
    blocks = v.reshape(v.shape[:-1] + (-1, 32))
    amax = np.abs(blocks).max(-1, keepdims=True)
    byte = np.maximum(np.where(amax > 0, np.frexp(amax)[1] - 1 + 127, 0) - down, 1)
    scale = np.exp2(byte - 127.0)
    codes = (blocks / scale).astype(np.float32).astype(dtype).astype(np.float64)
    return np.moveaxis((codes * scale).reshape(v.shape), -1, axis)


WIDE = False


def mx_kscale(k):
    if not WIDE:
        return np.ones(k)
    levels = np.array([10, -10, 5, -5, 0])
    if k % 512:
        return np.exp2(np.random.permutation(np.resize(levels, k // 32))).repeat(32)
    a = np.empty((k // 512, 16))
    for p in range(k // 512):
        a[p, :8] = np.random.permutation(np.resize(levels, 8))
        for g in range(8):
            far = levels[np.abs(levels - a[p, g]) >= 10]
            a[p, g + 8] = far[np.random.randint(len(far))]
    return np.exp2(a.ravel()).repeat(32)


BF16 = ml_dtypes.bfloat16


def bf(x):
    return np.asarray(x, np.float32).astype(BF16)


def f64(x):
    return np.asarray(x).astype(np.float64)


N, T, D, B0, C, P0, V1, P1, V2 = 2, 512, 1024, 2046, 2, 512, 2048, 512, 1024
MU = 0.25
SIG = 2.0


def softmax(v):
    e = np.exp(v - v.max(-1, keepdims=True))
    return e / e.sum(-1, keepdims=True)


def draw0():
    s, t = mx_kscale(D), mx_kscale(P0)
    hw = np.random.standard_normal((D, B0 + C)) * SIG / np.sqrt(D)
    hw[:, B0:] = hw[:, B0:] / SIG + (np.log(B0) + 0.5 * SIG * SIG) / (MU * D)
    return {"x": bf((np.random.standard_normal((N, T, D)) + MU) * s),
            "head_weight": bf(hw / s[:, None]),
            "tail_proj_0": bf(np.random.standard_normal((D, P0)) / np.sqrt(D) / s[:, None] * t),
            "tail_w_0": bf(np.random.standard_normal((P0, V1)) * SIG / np.sqrt(P0) / t[:, None])}


def core(x, head_weight, tail_proj_0, tail_w_0):
    xq = mxq(f64(x), 2, "e4m3")
    head_sm = softmax(xq @ mxq(f64(head_weight), 0, "e4m3"))
    h = xq @ mxq(f64(tail_proj_0), 0, "e4m3")
    tail_sm = softmax(mxq(h, 2, "e4m3") @ mxq(f64(tail_w_0), 0, "e4m3"))
    probs = np.concatenate([head_sm[..., :B0], tail_sm * head_sm[..., B0:B0 + 1]], axis=-1)
    return probs, head_sm[..., B0 + 1:B0 + C]


def e4m3fn_bytes(y):
    return np.clip(np.asarray(y, np.float64), -448.0, 448.0).astype(np.float32).astype(ml_dtypes.float8_e4m3fn).view(np.uint8)


def e4m3fn_values(b):
    return np.asarray(b, np.uint8).view(ml_dtypes.float8_e4m3fn).astype(np.float64)


def setup_inputs():
    d = draw0()
    x0 = np.asarray(d['head_weight']).astype(np.float64)
    s = (np.max(np.abs(x0), axis=(1,), keepdims=True) / 448.0).astype(np.float32)
    out = {}
    for k, v in d.items():
        if k == 'head_weight':
            out['head_weight_bytes'] = e4m3fn_bytes(x0 / s.astype(np.float64))
            out['head_weight_scale'] = s
        else:
            out[k] = v
    return out


def reference(x, head_weight_bytes, head_weight_scale, tail_proj_0, tail_w_0):
    return core(x, e4m3fn_values(head_weight_bytes) * head_weight_scale.astype(np.float64), tail_proj_0, tail_w_0)

@@ -1,0 +1,389 @@
+from contextlib import ExitStack
+
+import concourse.mybir as mybir
+from concourse.masks import make_identity
+
+F32 = mybir.dt.float32
+BF16 = mybir.dt.bfloat16
+U32 = mybir.dt.uint32
+U8 = mybir.dt.uint8
+FP8 = mybir.dt.float8_e4m3fn
+FP8X4 = mybir.dt.float8_e4m3fn_x4
+EXP = mybir.ActivationFunctionType.Exp
+MULT = mybir.AluOpType.mult
+ADD = mybir.AluOpType.add
+AX = mybir.AxisListType.X
+
+P = 128
+TILES = 8
+D_IN = 1024
+HEAD = 2048
+TOKENS_OUT = 2046
+H = 512
+TAIL = 2048
+ROW = 4094
+BANK = 512
+
+FLOPS = 2 * 1024 * (D_IN * HEAD + D_IN * H + H * TAIL)
+
+
+def carry(i):
+    return (ROW * i) % 8
+
+
+def down8(n):
+    return n - n % 8
+
+
+def up8(n):
+    return n + (-n) % 8
+
+
+def tile_adaptiveinputsoftmax_pa_kernel(tc, x, head_bytes, head_scale, tail_proj, tail_w, out_0, out_1):
+    nc = tc.nc
+    x_v = x.rearrange("a (q i) k -> (a q) i k", i=TILES)
+    hb_v = head_bytes.rearrange("(g p t) n -> p g t n", p=P, t=4)
+    sc_v = head_scale.rearrange("(g p t) o -> p g (t o)", p=P, t=4)
+    pr_v = tail_proj.rearrange("(g p t) c -> p g (t c)", p=P, t=4)
+    tw_v = tail_w.rearrange("(p t) n -> p t n", t=4)
+    out_v = out_0.rearrange("a (q i) c -> (a q) (i c)", i=TILES)
+    out1_v = out_1.rearrange("a (q i) o -> (a q) (i o)", i=TILES)
+
+    with ExitStack() as ctx:
+        keep = ctx.enter_context(tc.tile_pool(name="keep", bufs=1))
+        work = ctx.enter_context(tc.tile_pool(name="work", bufs=1))
+        psum = ctx.enter_context(tc.psum_pool(name="psum", bufs=8))
+
+        ident32 = keep.tile([P, P], F32, name="ident32", align_bytes=64)
+        ident16 = keep.tile([P, P], BF16, name="ident16", align_bytes=64)
+        scale = keep.tile([P, 2, 4], F32, name="scale")
+        hbytes = keep.tile([P, 2, 4, HEAD], U8, name="hbytes", align_bytes=64)
+        proj_raw = keep.tile([P, 2, 4 * H], BF16, name="proj_raw", align_bytes=64)
+        xc = keep.tile([P, TILES, 256], U32, name="xc", align_bytes=64)
+        xs = keep.tile([P, TILES, 256], U8, name="xs", align_bytes=64)
+        hc = keep.tile([P, 2, HEAD], U32, name="hc", align_bytes=64)
+        hs = keep.tile([P, 2, HEAD], U8, name="hs", align_bytes=64)
+        pc = keep.tile([P, 2, H], U32, name="pc", align_bytes=64)
+        ps = keep.tile([P, 2, H], U8, name="ps", align_bytes=64)
+        yc = keep.tile([P, TILES, P], U32, name="yc", align_bytes=64)
+        ys = keep.tile([P, TILES, P], U8, name="ys", align_bytes=64)
+        wc = keep.tile([P, TAIL], U32, name="wc", align_bytes=64)
+        ws = keep.tile([P, TAIL], U8, name="ws", align_bytes=64)
+        other = keep.tile([P, TILES], F32, name="other")
+        warm = keep.tile([P, 1], F32, name="warm")
+
+        x_raw = work.tile([P, TILES, D_IN], BF16, name="x_raw", tag="raw", bufs=1, align_bytes=64)
+
+        ctx.enter_context(tc.manual_schedule())
+
+        nc.sync.dma_start(out=scale[:], in_=sc_v)
+        for half in range(2):
+            for g in range(2):
+                cols = slice(1024 * half, 1024 * (half + 1))
+                if half == 0 and g == 0:
+                    nc.sync.dma_start(out=hbytes[:, g, 0:2, cols], in_=hb_v[:, g, 0:2, cols])
+                    nc.sync.dma_start(out=hbytes[:, g, 2:4, cols], in_=hb_v[:, g, 2:4, cols])
+                else:
+                    nc.sync.dma_start(out=hbytes[:, g, :, cols], in_=hb_v[:, g, :, cols])
+                i = 4 * half + 2 * g
+                nc.sync.dma_start(out=x_raw[:, i:i + 2, :], in_=x_v[:, i:i + 2, :])
+        for g in range(2):
+            nc.sync.dma_start(out=proj_raw[:, g, :], in_=pr_v[:, g, :])
+
+        nc.vector.memset(warm[:], 0.0)
+        nc.scalar.activation(out=warm[:], in_=warm[:], func=EXP)
+        make_identity(nc, ident32[:])
+        make_identity(nc, ident16[:])
+
+        wide = {}
+        hgrp = {}
+        xgrp = {}
+        pgrp = {}
+        wgrp = {}
+        ygrp = {}
+        tail_raw = {}
+
+        def widen(half, g):
+            if g == 0:
+                wide[half] = work.tile([P, 2, 4, 1024], BF16, name="wide", tag="row", bufs=5, align_bytes=64)
+            for t in range(4):
+                nc.vector.tensor_scalar(
+                    out=wide[half][:, g, t, :],
+                    in0=hbytes[:, g, t, 1024 * half:1024 * (half + 1)].bitcast(FP8),
+                    scalar1=scale[:, g, t:t + 1],
+                    scalar2=None,
+                    op0=MULT,
+                )
+
+        def weave(out, planes):
+            for b in range(2):
+                bank = psum.tile([P, 256, 4], BF16, name="bank", tag="bank", bufs=8)
+                for q in range(2):
+                    nc.tensor.matmul(
+                        out=bank[:, 128 * q:128 * (q + 1), :], lhsT=ident16[:], rhs=planes(2 * b + q), start=True, stop=True,
+                    )
+                nc.scalar.copy(
+                    out=out[:, 1024 * b:1024 * (b + 1)].bitcast(F32),
+                    in_=bank[:].rearrange("p n t -> p (n t)").bitcast(F32),
+                )
+
+        def weave_head(c, g):
+            hgrp[c, g] = work.tile([P, 2048], BF16, name="hgrp", tag="hgrp", bufs=4, align_bytes=64)
+            n0 = 512 * (c % 2)
+            weave(hgrp[c, g], lambda k: wide[c // 2][:, g, :, n0 + 128 * k:n0 + 128 * (k + 1)].rearrange("p t n -> p n t"))
+
+        def quant_head(c, g):
+            nc.vector.quantize_mx(
+                out=hc[:, g, c * BANK:(c + 1) * BANK].bitcast(FP8X4),
+                scales=hs[:, g, c * BANK:(c + 1) * BANK],
+                in_=hgrp[c, g][:],
+            )
+
+        def turn_x(i):
+            words = x_raw[:, i, :].bitcast(F32)
+            bank = psum.tile([P, 2, 2, P], F32, name="bank", tag="bank", bufs=8)
+            for g in range(2):
+                for u in range(2):
+                    nc.tensor.transpose(bank[:, g, u, :], words[:, 256 * g + u:256 * (g + 1):2], ident32[:])
+            if i % 2 == 0:
+                xgrp[i // 2] = work.tile([P, 2048], BF16, name="xgrp", tag="xgrp", bufs=3, align_bytes=64)
+            nc.scalar.copy(
+                out=xgrp[i // 2][:, 1024 * (i % 2):1024 * (i % 2 + 1)].bitcast(F32).rearrange("p (g r u) -> p g r u", g=2, u=2),
+                in_=bank[:].rearrange("p g u r -> p g r u"),
+            )
+
+        def quant_x(k):
+            nc.vector.quantize_mx(
+                out=xc[:, 2 * k:2 * k + 2, :].rearrange("p i w -> p (i w)").bitcast(FP8X4),
+                scales=xs[:, 2 * k:2 * k + 2, :].rearrange("p i w -> p (i w)"),
+                in_=xgrp[k][:],
+            )
+
+        def weave_proj(g):
+            pgrp[g] = work.tile([P, 2048], BF16, name="pgrp", tag="pgrp", bufs=2, align_bytes=64)
+            view = proj_raw[:, g, :].rearrange("p (j m t) -> p t m j", j=4, t=4)
+            weave(pgrp[g], lambda k: view[:, k, :, :])
+
+        def quant_proj(g):
+            nc.vector.quantize_mx(out=pc[:, g, :].bitcast(FP8X4), scales=ps[:, g, :], in_=pgrp[g][:])
+
+        def load_tail():
+            tail_raw[0] = work.tile([P, 4, TAIL], BF16, name="tail_raw", tag="raw", bufs=1, align_bytes=64)
+            for d in range(2):
+                nc.sync.dma_start(out=tail_raw[0][:, :, 1024 * d:1024 * (d + 1)], in_=tw_v[:, :, 1024 * d:1024 * (d + 1)])
+
+        def weave_tail(d):
+            wgrp[d] = work.tile([P, 2048], BF16, name="wgrp", tag="wgrp", bufs=2, align_bytes=64)
+            if d == 0:
+                weave(wgrp[d], lambda k: tail_raw[0][:, :, 128 * k:128 * (k + 1)].rearrange("p t n -> p n t"))
+                return
+            nc.vector.tensor_copy(
+                out=wgrp[d][:].rearrange("p (c i t) -> p c t i", i=4, t=4),
+                in_=tail_raw[0][:, :, BANK * d:BANK * (d + 1)].rearrange("p t (c i) -> p c t i", i=4),
+            )
+
+        def quant_tail(d):
+            nc.vector.quantize_mx(
+                out=wc[:, BANK * d:BANK * (d + 1)].bitcast(FP8X4),
+                scales=ws[:, BANK * d:BANK * (d + 1)],
+                in_=wgrp[d][:],
+            )
+
+        def make_y(i):
+            bank = psum.tile([P, 4, P], F32, name="bank", tag="bank", bufs=8)
+            for t in range(4):
+                for g in range(2):
+                    nc.tensor.matmul_mx(
+                        out=bank[:, t, :],
+                        lhsT=pc[:, g, P * t:P * (t + 1)].bitcast(FP8X4),
+                        lhsT_scale=ps[:, g, P * t:P * (t + 1)],
+                        rhs=xc[:, i, P * g:P * (g + 1)].bitcast(FP8X4),
+                        rhs_scale=xs[:, i, P * g:P * (g + 1)],
+                        start=(g == 0),
+                        stop=(g == 1),
+                    )
+            if i % 2 == 0:
+                ygrp[i // 2] = work.tile([P, 2, P, 4], BF16, name="ygrp", tag="ygrp", bufs=2, align_bytes=64)
+            nc.scalar.copy(out=ygrp[i // 2][:, i % 2], in_=bank[:].rearrange("p t n -> p n t"))
+
+        def quant_y(k):
+            nc.vector.quantize_mx(
+                out=yc[:, 2 * k:2 * k + 2, :].rearrange("p i n -> p (i n)").bitcast(FP8X4),
+                scales=ys[:, 2 * k:2 * k + 2, :].rearrange("p i n -> p (i n)"),
+                in_=ygrp[k][:].rearrange("p i n t -> p (i n t)"),
+            )
+
+        rows = {}
+        state = {}
+
+        def logits(kind, i):
+            banks = []
+            for c in range(4):
+                bank = psum.tile([P, BANK], F32, name="bank", tag="bank", bufs=8)
+                cols = slice(BANK * c, BANK * (c + 1))
+                if kind == "h":
+                    for g in range(2):
+                        nc.tensor.matmul_mx(
+                            out=bank[:],
+                            lhsT=xc[:, i, P * g:P * (g + 1)].bitcast(FP8X4),
+                            lhsT_scale=xs[:, i, P * g:P * (g + 1)],
+                            rhs=hc[:, g, cols].bitcast(FP8X4),
+                            rhs_scale=hs[:, g, cols],
+                            start=(g == 0),
+                            stop=(g == 1),
+                        )
+                else:
+                    nc.tensor.matmul_mx(
+                        out=bank[:],
+                        lhsT=yc[:, i, :].bitcast(FP8X4),
+                        lhsT_scale=ys[:, i, :],
+                        rhs=wc[:, cols].bitcast(FP8X4),
+                        rhs_scale=ws[:, cols],
+                        start=True,
+                        stop=True,
+                    )
+                banks.append(bank)
+            return banks
+
+        def finish(group):
+            sums = state[group[0]]["sums"]
+            k0 = state[group[0]]["slot"]
+            total = work.tile([P, 2], F32, name="total", tag="total", bufs=4)
+            inv = work.tile([P, 2], F32, name="inv", tag="inv", bufs=6)
+            m = len(group)
+            nc.vector.tensor_reduce(out=total[:, 0:m], in_=sums[:, k0:k0 + m, :], axis=AX, op=ADD)
+            nc.vector.reciprocal(out=inv[:, 0:m], in_=total[:, 0:m])
+            for k, (kind, i) in enumerate(group):
+                scale_out(kind, i, inv[:, k:k + 1])
+
+        def scale_out(kind, i, inv):
+            row, c0 = rows[i], carry(i)
+            last = i == TILES - 1
+            split = down8(c0 + TOKENS_OUT)
+            if kind == "h":
+                nc.gpsimd.tensor_scalar(out=row[:, c0:c0 + TOKENS_OUT], in0=row[:, c0:c0 + TOKENS_OUT], scalar1=inv, scalar2=0.0, op0=MULT, op1=ADD)
+                clus = state[kind, i]["clus"]
+                prob = work.tile([P, 1], F32, name="prob", tag="prob", bufs=6)
+                nc.gpsimd.tensor_scalar(out=prob[:], in0=clus[:, 0:1], scalar1=inv, scalar2=0.0, op0=MULT, op1=ADD)
+                nc.gpsimd.tensor_scalar(out=other[:, i:i + 1], in0=clus[:, 1:2], scalar1=inv, scalar2=0.0, op0=MULT, op1=ADD)
+                state["prob", i] = prob
+                nc.sync.dma_start(out=out_v[:, ROW * i - c0 + up8(c0):ROW * i - c0 + split], in_=row[:, up8(c0):split])
+                if last:
+                    nc.sync.dma_start(out=out1_v, in_=other[:])
+            else:
+                prob = state["prob", i]
+                base = c0 + TOKENS_OUT
+                end = c0 + ROW
+                if not last:
+                    engine = nc.vector if i == TILES - 2 else nc.gpsimd
+                    engine.tensor_scalar(
+                        out=row[:, base:end], in0=row[:, base:end], scalar1=inv, scalar2=prob[:], op0=MULT, op1=MULT,
+                    )
+                    if up8(end) > end:
+                        c1 = carry(i + 1)
+                        engine.tensor_copy(out=row[:, end:up8(end)], in_=rows[i + 1][:, c1:8])
+                    nc.sync.dma_start(out=out_v[:, ROW * i - c0 + split:ROW * i - c0 + up8(end)], in_=row[:, split:up8(end)])
+                else:
+                    for a in range(0, TAIL, 512):
+                        nc.vector.tensor_scalar(
+                            out=row[:, base + a:base + a + 512], in0=row[:, base + a:base + a + 512],
+                            scalar1=inv, scalar2=prob[:], op0=MULT, op1=MULT,
+                        )
+                        nc.sync.dma_start(out=out_v[:, ROW * i + TOKENS_OUT + a:ROW * i + TOKENS_OUT + a + 512], in_=row[:, base + a:base + a + 512])
+
+        SEQ = [("h", 0), ("h", 1), ("h", 2), ("t", 0), ("h", 3), ("t", 1), ("h", 4), ("t", 2), ("h", 5), ("t", 3), ("h", 6), ("t", 4), ("h", 7), ("t", 5), ("t", 6), ("t", 7)]
+
+        GROUPS = {6: SEQ[3:5], 8: SEQ[5:7], 10: SEQ[7:9], 12: SEQ[9:11], 14: SEQ[11:13], 15: SEQ[13:14]}
+
+        def block(n):
+            kind, i = SEQ[n]
+            st = {}
+            state[kind, i] = st
+            if kind == "h":
+                rows[i] = work.tile([P, 4104], F32, name="row", tag="row", bufs=5, align_bytes=64)
+            banks = logits(kind, i)
+            peaks = work.tile([P, 4], F32, name="peaks", tag="peaks", bufs=4)
+            for c in range(4):
+                nc.vector.tensor_reduce(out=peaks[:, c:c + 1], in_=banks[c][:], axis=AX, op=mybir.AluOpType.max)
+                if c == 0 and n in GROUPS:
+                    finish(GROUPS[n])
+            negmax = work.tile([P, 1], F32, name="negmax", tag="negmax", bufs=4)
+            nc.vector.tensor_reduce(out=negmax[:], in_=peaks[:], axis=AX, op=mybir.AluOpType.max, negate=True)
+            if n % 2 == 1 or n == 0:
+                st["sums"] = work.tile([P, 2, 4], F32, name="sums4", tag="sums4", bufs=4)
+            else:
+                st["sums"] = state[SEQ[n - 1]]["sums"]
+            st["slot"] = (n + 1) % 2 if n else 0
+            start = carry(i) + (0 if kind == "h" else TOKENS_OUT)
+            for c in range(4):
+                nc.scalar.activation(
+                    out=rows[i][:, start + BANK * c:start + BANK * (c + 1)], in_=banks[c][:], func=EXP,
+                    bias=negmax[:], scale=1.0, accum_out=st["sums"][:, st["slot"], c:c + 1],
+                )
+            if kind == "h":
+                st["clus"] = work.tile([P, 2], F32, name="clus", tag="clus", bufs=5)
+                nc.scalar.copy(out=st["clus"][:], in_=rows[i][:, start + TOKENS_OUT:start + HEAD])
+
+        widen(0, 0)
+        turn_x(0)
+        turn_x(1)
+        weave_head(0, 0)
+        weave_head(1, 0)
+        widen(0, 1)
+        quant_x(0)
+        turn_x(2)
+        turn_x(3)
+        weave_head(0, 1)
+        weave_head(1, 1)
+        quant_head(0, 0)
+        quant_head(1, 0)
+        widen(1, 0)
+        quant_x(1)
+        turn_x(4)
+        turn_x(5)
+        weave_head(2, 0)
+        weave_head(3, 0)
+        quant_head(0, 1)
+        quant_head(1, 1)
+        widen(1, 1)
+        quant_x(2)
+        turn_x(6)
+        turn_x(7)
+        load_tail()
+        weave_head(2, 1)
+        weave_head(3, 1)
+        weave_proj(0)
+        weave_proj(1)
+        quant_head(2, 0)
+        quant_head(3, 0)
+        quant_x(3)
+        quant_head(2, 1)
+        quant_head(3, 1)
+        quant_proj(0)
+        quant_proj(1)
+        block(0)
+        weave_tail(0)
+        for i in range(4):
+            make_y(i)
+        weave_tail(1)
+        quant_tail(0)
+        finish(SEQ[0:1])
+        block(1)
+        for i in range(4, 8):
+            make_y(i)
+        quant_tail(1)
+        quant_y(0)
+        quant_y(1)
+        weave_tail(2)
+        finish(SEQ[1:2])
+        block(2)
+        weave_tail(3)
+        quant_tail(2)
+        quant_y(2)
+        quant_y(3)
+        quant_tail(3)
+        finish(SEQ[2:3])
+        for n in range(3, 16):
+            block(n)
+        finish(SEQ[14:15])
+        finish(SEQ[15:16])

@@ -10,6 +10,7 @@ U8 = mybir.dt.uint8
 FP8 = mybir.dt.float8_e4m3fn
 FP8X4 = mybir.dt.float8_e4m3fn_x4
 EXP = mybir.ActivationFunctionType.Exp
+COPY = mybir.ActivationFunctionType.Copy
 MULT = mybir.AluOpType.mult
 ADD = mybir.AluOpType.add
 AX = mybir.AxisListType.X
@@ -53,12 +54,11 @@ def tile_adaptiveinputsoftmax_pa_kernel(tc, x, head_bytes, head_scale, tail_proj
         keep = ctx.enter_context(tc.tile_pool(name="keep", bufs=1))
         work = ctx.enter_context(tc.tile_pool(name="work", bufs=1))
         psum = ctx.enter_context(tc.psum_pool(name="psum", bufs=8))
+        late = {}
 
         ident32 = keep.tile([P, P], F32, name="ident32", align_bytes=64)
         ident16 = keep.tile([P, P], BF16, name="ident16", align_bytes=64)
         scale = keep.tile([P, 2, 4], F32, name="scale")
-        hbytes = keep.tile([P, 2, 4, HEAD], U8, name="hbytes", align_bytes=64)
-        proj_raw = keep.tile([P, 2, 4 * H], BF16, name="proj_raw", align_bytes=64)
         xc = keep.tile([P, TILES, 256], U32, name="xc", align_bytes=64)
         xs = keep.tile([P, TILES, 256], U8, name="xs", align_bytes=64)
         hc = keep.tile([P, 2, HEAD], U32, name="hc", align_bytes=64)
@@ -70,50 +70,33 @@ def tile_adaptiveinputsoftmax_pa_kernel(tc, x, head_bytes, head_scale, tail_proj
         wc = keep.tile([P, TAIL], U32, name="wc", align_bytes=64)
         ws = keep.tile([P, TAIL], U8, name="ws", align_bytes=64)
         other = keep.tile([P, TILES], F32, name="other")
+        pair = keep.tile([P, TILES, 2], F32, name="pair")
         warm = keep.tile([P, 1], F32, name="warm")
 
-        x_raw = work.tile([P, TILES, D_IN], BF16, name="x_raw", tag="raw", bufs=1, align_bytes=64)
+        tail_raw = keep.tile([P, 4, TAIL], BF16, name="tail_raw", align_bytes=64)
 
         ctx.enter_context(tc.manual_schedule())
 
-        nc.sync.dma_start(out=scale[:], in_=sc_v)
-        for half in range(2):
-            for g in range(2):
-                cols = slice(1024 * half, 1024 * (half + 1))
-                if half == 0 and g == 0:
-                    nc.sync.dma_start(out=hbytes[:, g, 0:2, cols], in_=hb_v[:, g, 0:2, cols])
-                    nc.sync.dma_start(out=hbytes[:, g, 2:4, cols], in_=hb_v[:, g, 2:4, cols])
-                else:
-                    nc.sync.dma_start(out=hbytes[:, g, :, cols], in_=hb_v[:, g, :, cols])
-                i = 4 * half + 2 * g
-                nc.sync.dma_start(out=x_raw[:, i:i + 2, :], in_=x_v[:, i:i + 2, :])
-        for g in range(2):
-            nc.sync.dma_start(out=proj_raw[:, g, :], in_=pr_v[:, g, :])
-
-        nc.vector.memset(warm[:], 0.0)
-        nc.scalar.activation(out=warm[:], in_=warm[:], func=EXP)
-        make_identity(nc, ident32[:])
-        make_identity(nc, ident16[:])
-
+        MODE = {("proj",0):"S",("proj",1):"S",("tail",0):"S"}
+        WIDEN_S = {(h,g,t) for h in range(2) for g in range(2) for t in (2,3)}
         wide = {}
         hgrp = {}
         xgrp = {}
         pgrp = {}
         wgrp = {}
         ygrp = {}
-        tail_raw = {}
 
         def widen(half, g):
             if g == 0:
-                wide[half] = work.tile([P, 2, 4, 1024], BF16, name="wide", tag="row", bufs=5, align_bytes=64)
+                wide[half] = work.tile([P, 2, 4, 1024], BF16, name="wide", tag="row", bufs=4, align_bytes=64)
             for t in range(4):
-                nc.vector.tensor_scalar(
-                    out=wide[half][:, g, t, :],
-                    in0=hbytes[:, g, t, 1024 * half:1024 * (half + 1)].bitcast(FP8),
-                    scalar1=scale[:, g, t:t + 1],
-                    scalar2=None,
-                    op0=MULT,
-                )
+                codes = hbytes[:, g, t, 1024 * half:1024 * (half + 1)].bitcast(FP8)
+                if (half, g, t) in WIDEN_S:
+                    nc.scalar.activation(out=wide[half][:, g, t, :], in_=codes, func=COPY, scale=scale[:, g, t:t + 1])
+                else:
+                    nc.vector.tensor_scalar(
+                        out=wide[half][:, g, t, :], in0=codes, scalar1=scale[:, g, t:t + 1], scalar2=None, op0=MULT,
+                    )
 
         def weave(out, planes):
             for b in range(2):
@@ -128,8 +111,15 @@ def tile_adaptiveinputsoftmax_pa_kernel(tc, x, head_bytes, head_scale, tail_proj
                 )
 
         def weave_head(c, g):
-            hgrp[c, g] = work.tile([P, 2048], BF16, name="hgrp", tag="hgrp", bufs=4, align_bytes=64)
+            hgrp[c, g] = early.tile([P, 2048], BF16, name="hgrp", tag="hgrp", bufs=4, align_bytes=64)
             n0 = 512 * (c % 2)
+            if MODE.get(("head", c, g)) != "T":
+                copy = nc.scalar.copy if MODE.get(("head", c, g)) == "S" else nc.vector.tensor_copy
+                copy(
+                    out=hgrp[c, g][:].rearrange("p (c i t) -> p c t i", i=4, t=4),
+                    in_=wide[c // 2][:, g, :, n0:n0 + 512].rearrange("p t (c i) -> p c t i", i=4),
+                )
+                return
             weave(hgrp[c, g], lambda k: wide[c // 2][:, g, :, n0 + 128 * k:n0 + 128 * (k + 1)].rearrange("p t n -> p n t"))
 
         def quant_head(c, g):
@@ -146,7 +136,7 @@ def tile_adaptiveinputsoftmax_pa_kernel(tc, x, head_bytes, head_scale, tail_proj
                 for u in range(2):
                     nc.tensor.transpose(bank[:, g, u, :], words[:, 256 * g + u:256 * (g + 1):2], ident32[:])
             if i % 2 == 0:
-                xgrp[i // 2] = work.tile([P, 2048], BF16, name="xgrp", tag="xgrp", bufs=3, align_bytes=64)
+                xgrp[i // 2] = early.tile([P, 2048], BF16, name="xgrp", tag="xgrp", bufs=3, align_bytes=64)
             nc.scalar.copy(
                 out=xgrp[i // 2][:, 1024 * (i % 2):1024 * (i % 2 + 1)].bitcast(F32).rearrange("p (g r u) -> p g r u", g=2, u=2),
                 in_=bank[:].rearrange("p g u r -> p g r u"),
@@ -160,26 +150,26 @@ def tile_adaptiveinputsoftmax_pa_kernel(tc, x, head_bytes, head_scale, tail_proj
             )
 
         def weave_proj(g):
-            pgrp[g] = work.tile([P, 2048], BF16, name="pgrp", tag="pgrp", bufs=2, align_bytes=64)
+            pgrp[g] = early.tile([P, 2048], BF16, name="pgrp", tag="pgrp", bufs=2, align_bytes=64)
             view = proj_raw[:, g, :].rearrange("p (j m t) -> p t m j", j=4, t=4)
+            if MODE.get(("proj", g)) != "T":
+                copy = nc.scalar.copy if MODE.get(("proj", g)) == "S" else nc.vector.tensor_copy
+                copy(out=pgrp[g][:].rearrange("p (t m j) -> p t m j", t=4, j=4), in_=view)
+                return
             weave(pgrp[g], lambda k: view[:, k, :, :])
 
         def quant_proj(g):
             nc.vector.quantize_mx(out=pc[:, g, :].bitcast(FP8X4), scales=ps[:, g, :], in_=pgrp[g][:])
 
-        def load_tail():
-            tail_raw[0] = work.tile([P, 4, TAIL], BF16, name="tail_raw", tag="raw", bufs=1, align_bytes=64)
-            for d in range(2):
-                nc.sync.dma_start(out=tail_raw[0][:, :, 1024 * d:1024 * (d + 1)], in_=tw_v[:, :, 1024 * d:1024 * (d + 1)])
-
         def weave_tail(d):
             wgrp[d] = work.tile([P, 2048], BF16, name="wgrp", tag="wgrp", bufs=2, align_bytes=64)
-            if d == 0:
-                weave(wgrp[d], lambda k: tail_raw[0][:, :, 128 * k:128 * (k + 1)].rearrange("p t n -> p n t"))
+            if MODE.get(("tail", d)) == "T":
+                weave(wgrp[d], lambda k: tail_raw[:, :, 128 * k:128 * (k + 1)].rearrange("p t n -> p n t"))
                 return
-            nc.vector.tensor_copy(
+            copy = nc.scalar.copy if MODE.get(("tail", d)) == "S" else nc.vector.tensor_copy
+            copy(
                 out=wgrp[d][:].rearrange("p (c i t) -> p c t i", i=4, t=4),
-                in_=tail_raw[0][:, :, BANK * d:BANK * (d + 1)].rearrange("p t (c i) -> p c t i", i=4),
+                in_=tail_raw[:, :, BANK * d:BANK * (d + 1)].rearrange("p t (c i) -> p c t i", i=4),
             )
 
         def quant_tail(d):
@@ -245,14 +235,18 @@ def tile_adaptiveinputsoftmax_pa_kernel(tc, x, head_bytes, head_scale, tail_proj
                 banks.append(bank)
             return banks
 
-        def finish(group):
+        def add_up(group):
             sums = state[group[0]]["sums"]
             k0 = state[group[0]]["slot"]
             total = work.tile([P, 2], F32, name="total", tag="total", bufs=4)
-            inv = work.tile([P, 2], F32, name="inv", tag="inv", bufs=6)
             m = len(group)
             nc.vector.tensor_reduce(out=total[:, 0:m], in_=sums[:, k0:k0 + m, :], axis=AX, op=ADD)
-            nc.vector.reciprocal(out=inv[:, 0:m], in_=total[:, 0:m])
+            state["total", group[0]] = total
+
+        def finish(group):
+            m = len(group)
+            inv = work.tile([P, 2], F32, name="inv", tag="inv", bufs=6)
+            nc.vector.reciprocal(out=inv[:, 0:m], in_=state["total", group[0]][:, 0:m])
             for k, (kind, i) in enumerate(group):
                 scale_out(kind, i, inv[:, k:k + 1])
 
@@ -261,23 +255,22 @@ def tile_adaptiveinputsoftmax_pa_kernel(tc, x, head_bytes, head_scale, tail_proj
             last = i == TILES - 1
             split = down8(c0 + TOKENS_OUT)
             if kind == "h":
-                nc.gpsimd.tensor_scalar(out=row[:, c0:c0 + TOKENS_OUT], in0=row[:, c0:c0 + TOKENS_OUT], scalar1=inv, scalar2=0.0, op0=MULT, op1=ADD)
+                engine = nc.vector if ("h", i) in ON_VECTOR else nc.gpsimd
+                engine.tensor_scalar(out=row[:, c0:c0 + TOKENS_OUT], in0=row[:, c0:c0 + TOKENS_OUT], scalar1=inv, scalar2=0.0, op0=MULT, op1=ADD)
                 clus = state[kind, i]["clus"]
-                prob = work.tile([P, 1], F32, name="prob", tag="prob", bufs=6)
-                nc.gpsimd.tensor_scalar(out=prob[:], in0=clus[:, 0:1], scalar1=inv, scalar2=0.0, op0=MULT, op1=ADD)
-                nc.gpsimd.tensor_scalar(out=other[:, i:i + 1], in0=clus[:, 1:2], scalar1=inv, scalar2=0.0, op0=MULT, op1=ADD)
-                state["prob", i] = prob
+                nc.gpsimd.tensor_scalar(out=pair[:, i, :], in0=clus[:], scalar1=inv, scalar2=0.0, op0=MULT, op1=ADD)
                 nc.sync.dma_start(out=out_v[:, ROW * i - c0 + up8(c0):ROW * i - c0 + split], in_=row[:, up8(c0):split])
                 if last:
+                    nc.gpsimd.tensor_copy(out=other[:], in_=pair[:, :, 1])
                     nc.sync.dma_start(out=out1_v, in_=other[:])
             else:
-                prob = state["prob", i]
+                prob = pair[:, i, 0:1]
                 base = c0 + TOKENS_OUT
                 end = c0 + ROW
                 if not last:
-                    engine = nc.vector if i == TILES - 2 else nc.gpsimd
+                    engine = nc.vector if ("t", i) in ON_VECTOR else nc.gpsimd
                     engine.tensor_scalar(
-                        out=row[:, base:end], in0=row[:, base:end], scalar1=inv, scalar2=prob[:], op0=MULT, op1=MULT,
+                        out=row[:, base:end], in0=row[:, base:end], scalar1=inv, scalar2=prob, op0=MULT, op1=MULT,
                     )
                     if up8(end) > end:
                         c1 = carry(i + 1)
@@ -287,103 +280,150 @@ def tile_adaptiveinputsoftmax_pa_kernel(tc, x, head_bytes, head_scale, tail_proj
                     for a in range(0, TAIL, 512):
                         nc.vector.tensor_scalar(
                             out=row[:, base + a:base + a + 512], in0=row[:, base + a:base + a + 512],
-                            scalar1=inv, scalar2=prob[:], op0=MULT, op1=MULT,
+                            scalar1=inv, scalar2=prob, op0=MULT, op1=MULT,
                         )
                         nc.sync.dma_start(out=out_v[:, ROW * i + TOKENS_OUT + a:ROW * i + TOKENS_OUT + a + 512], in_=row[:, base + a:base + a + 512])
 
-        SEQ = [("h", 0), ("h", 1), ("h", 2), ("t", 0), ("h", 3), ("t", 1), ("h", 4), ("t", 2), ("h", 5), ("t", 3), ("h", 6), ("t", 4), ("h", 7), ("t", 5), ("t", 6), ("t", 7)]
+        SEQ = [("h", 0), ("h", 1), ("h", 2), ("h", 3), ("t", 0), ("h", 4), ("t", 1), ("h", 5), ("t", 2), ("h", 6), ("t", 3), ("h", 7), ("t", 4), ("t", 5), ("t", 6), ("t", 7)]
 
-        GROUPS = {6: SEQ[3:5], 8: SEQ[5:7], 10: SEQ[7:9], 12: SEQ[9:11], 14: SEQ[11:13], 15: SEQ[13:14]}
+        ON_VECTOR = {("h", 0), ("t", 5), ("t", 6)}
+        GROUPS = {4: SEQ[2:3], 5: SEQ[3:4], 7: SEQ[4:6], 9: SEQ[6:8], 11: SEQ[8:10], 13: SEQ[10:12], 15: SEQ[12:13]}
 
-        def block(n):
+        def peaks(n, then=()):
             kind, i = SEQ[n]
             st = {}
             state[kind, i] = st
-            if kind == "h":
-                rows[i] = work.tile([P, 4104], F32, name="row", tag="row", bufs=5, align_bytes=64)
-            banks = logits(kind, i)
-            peaks = work.tile([P, 4], F32, name="peaks", tag="peaks", bufs=4)
+            st["banks"] = logits(kind, i)
+            st["peaks"] = work.tile([P, 4], F32, name="peaks", tag="peaks", bufs=4)
             for c in range(4):
-                nc.vector.tensor_reduce(out=peaks[:, c:c + 1], in_=banks[c][:], axis=AX, op=mybir.AluOpType.max)
-                if c == 0 and n in GROUPS:
-                    finish(GROUPS[n])
+                nc.vector.tensor_reduce(out=st["peaks"][:, c:c + 1], in_=st["banks"][c][:], axis=AX, op=mybir.AluOpType.max)
+                if c < len(then):
+                    then[c]()
+
+        def exps(n):
+            kind, i = SEQ[n]
+            st = state[kind, i]
+            if kind == "h":
+                if 4 <= i < 7:
+                    rows[i] = late["pool"].tile([P, 4104], F32, name="late_row", tag="late_row", bufs=3, align_bytes=64)
+                else:
+                    rows[i] = work.tile([P, 4104], F32, name="row", tag="row", bufs=4, align_bytes=64)
             negmax = work.tile([P, 1], F32, name="negmax", tag="negmax", bufs=4)
-            nc.vector.tensor_reduce(out=negmax[:], in_=peaks[:], axis=AX, op=mybir.AluOpType.max, negate=True)
-            if n % 2 == 1 or n == 0:
+            nc.vector.tensor_reduce(out=negmax[:], in_=st["peaks"][:], axis=AX, op=mybir.AluOpType.max, negate=True)
+            if n % 2 == 0:
                 st["sums"] = work.tile([P, 2, 4], F32, name="sums4", tag="sums4", bufs=4)
             else:
                 st["sums"] = state[SEQ[n - 1]]["sums"]
-            st["slot"] = (n + 1) % 2 if n else 0
+            st["slot"] = n % 2
             start = carry(i) + (0 if kind == "h" else TOKENS_OUT)
             for c in range(4):
                 nc.scalar.activation(
-                    out=rows[i][:, start + BANK * c:start + BANK * (c + 1)], in_=banks[c][:], func=EXP,
+                    out=rows[i][:, start + BANK * c:start + BANK * (c + 1)], in_=st["banks"][c][:], func=EXP,
                     bias=negmax[:], scale=1.0, accum_out=st["sums"][:, st["slot"], c:c + 1],
                 )
             if kind == "h":
                 st["clus"] = work.tile([P, 2], F32, name="clus", tag="clus", bufs=5)
                 nc.scalar.copy(out=st["clus"][:], in_=rows[i][:, start + TOKENS_OUT:start + HEAD])
 
-        widen(0, 0)
-        turn_x(0)
-        turn_x(1)
-        weave_head(0, 0)
-        weave_head(1, 0)
-        widen(0, 1)
-        quant_x(0)
-        turn_x(2)
-        turn_x(3)
-        weave_head(0, 1)
-        weave_head(1, 1)
-        quant_head(0, 0)
-        quant_head(1, 0)
-        widen(1, 0)
-        quant_x(1)
-        turn_x(4)
-        turn_x(5)
-        weave_head(2, 0)
-        weave_head(3, 0)
-        quant_head(0, 1)
-        quant_head(1, 1)
-        widen(1, 1)
-        quant_x(2)
-        turn_x(6)
-        turn_x(7)
-        load_tail()
-        weave_head(2, 1)
-        weave_head(3, 1)
-        weave_proj(0)
-        weave_proj(1)
-        quant_head(2, 0)
-        quant_head(3, 0)
-        quant_x(3)
-        quant_head(2, 1)
-        quant_head(3, 1)
-        quant_proj(0)
-        quant_proj(1)
-        block(0)
-        weave_tail(0)
+        with tc.tile_pool(name="early", bufs=1) as early:
+            hbytes = early.tile([P, 2, 4, HEAD], U8, name="hbytes", align_bytes=64)
+            proj_raw = early.tile([P, 2, 4 * H], BF16, name="proj_raw", align_bytes=64)
+            x_raw = early.tile([P, TILES, D_IN], BF16, name="x_raw", align_bytes=64)
+            nc.sync.dma_start(out=scale[:], in_=sc_v)
+            for half in range(2):
+                for g in range(2):
+                    cols = slice(1024 * half, 1024 * (half + 1))
+                    if half == 0 and g == 0:
+                        nc.sync.dma_start(out=hbytes[:, g, 0:2, cols], in_=hb_v[:, g, 0:2, cols])
+                        nc.sync.dma_start(out=hbytes[:, g, 2:4, cols], in_=hb_v[:, g, 2:4, cols])
+                    else:
+                        nc.sync.dma_start(out=hbytes[:, g, :, cols], in_=hb_v[:, g, :, cols])
+                    i = 4 * half + 2 * g
+                    nc.sync.dma_start(out=x_raw[:, i:i + 2, :], in_=x_v[:, i:i + 2, :])
+            for g in range(2):
+                nc.sync.dma_start(out=proj_raw[:, g, :], in_=pr_v[:, g, :])
+            for d in range(2):
+                nc.sync.dma_start(out=tail_raw[:, :, 1024 * d:1024 * (d + 1)], in_=tw_v[:, :, 1024 * d:1024 * (d + 1)])
+
+            nc.vector.memset(warm[:], 0.0)
+            nc.scalar.activation(out=warm[:], in_=warm[:], func=EXP)
+            make_identity(nc, ident32[:])
+            make_identity(nc, ident16[:])
+
+            widen(0, 0)
+            turn_x(0)
+            turn_x(1)
+            weave_head(0, 0)
+            weave_head(1, 0)
+            widen(0, 1)
+            quant_x(0)
+            turn_x(2)
+            turn_x(3)
+            weave_head(0, 1)
+            weave_head(1, 1)
+            quant_head(0, 0)
+            quant_head(1, 0)
+            widen(1, 0)
+            quant_x(1)
+            turn_x(4)
+            turn_x(5)
+            weave_head(2, 0)
+            weave_head(3, 0)
+            quant_head(0, 1)
+            quant_head(1, 1)
+            widen(1, 1)
+            quant_x(2)
+            turn_x(6)
+            turn_x(7)
+            weave_proj(0)
+            weave_head(2, 1)
+            weave_head(3, 1)
+            weave_proj(1)
+            quant_head(2, 0)
+            quant_head(3, 0)
+            quant_x(3)
+            quant_proj(0)
+            weave_tail(0)
+            quant_head(2, 1)
+            quant_head(3, 1)
+            quant_proj(1)
+        late["pool"] = ctx.enter_context(tc.tile_pool(name="late", bufs=1))
+        peaks(0)
+        peaks(1, [lambda: exps(0)])
         for i in range(4):
             make_y(i)
         weave_tail(1)
+        exps(1)
         quant_tail(0)
-        finish(SEQ[0:1])
-        block(1)
-        for i in range(4, 8):
-            make_y(i)
-        quant_tail(1)
-        quant_y(0)
-        quant_y(1)
         weave_tail(2)
-        finish(SEQ[1:2])
-        block(2)
+        add_up(SEQ[0:1])
+        quant_tail(1)
+        finish(SEQ[0:1])
         weave_tail(3)
         quant_tail(2)
+        for i in range(4, 8):
+            make_y(i)
+        quant_y(0)
+        add_up(SEQ[1:2])
+        quant_tail(3)
+        finish(SEQ[1:2])
+        peaks(2)
+        quant_y(1)
+        exps(2)
         quant_y(2)
         quant_y(3)
-        quant_tail(3)
-        finish(SEQ[2:3])
         for n in range(3, 16):
-            block(n)
+            group = GROUPS.get(n)
+            then = []
+            if n > 3:
+                then.append(lambda: exps(n - 1))
+            if group:
+                then += [lambda: add_up(group), lambda: finish(group)]
+            peaks(n, then)
+        exps(15)
+        add_up(SEQ[13:14])
+        finish(SEQ[13:14])
+        add_up(SEQ[14:15])
         finish(SEQ[14:15])
+        add_up(SEQ[15:16])
         finish(SEQ[15:16])

@@ -13,6 +13,7 @@ EXP = mybir.ActivationFunctionType.Exp
 COPY = mybir.ActivationFunctionType.Copy
 MULT = mybir.AluOpType.mult
 ADD = mybir.AluOpType.add
+MAX = mybir.AluOpType.max
 AX = mybir.AxisListType.X
 
 P = 128
@@ -26,6 +27,31 @@ ROW = 4094
 BANK = 512
 
 FLOPS = 2 * 1024 * (D_IN * HEAD + D_IN * H + H * TAIL)
+
+SEQ = [('h', 0), ('h', 1), ('h', 2), ('h', 3), ('h', 4), ('t', 0), ('h', 5), ('t', 1), ('h', 6), ('t', 2), ('h', 7), ('t', 3), ('t', 4), ('t', 5), ('t', 6), ('t', 7)]
+UNITS = {('h', 0, 0): 'T', ('h', 0, 1): 'V', ('h', 1, 0): 'T', ('h', 1, 1): 'V', ('h', 2, 0): 'V', ('h', 2, 1): 'S', ('h', 3, 0): 'V', ('h', 3, 1): 'V', ('p', 0): 'T', ('p', 1): 'G', ('t', 0): 'T', ('t', 1): 'S', ('t', 2): 'G', ('t', 3): 'G'}
+WIDEN_S = {(1, 0, 1), (1, 1, 0), (0, 0, 2), (0, 1, 2), (1, 0, 2)}
+ON_VECTOR = {('t', 3), ('t', 5), ('t', 6), ('t', 7)}
+X_V = ()
+Y_V = {1}
+HBUFS = 4
+XBUFS = 3
+PLAN_EARLY = """
+w:0:0 w:0:1 u:h:0:1 x:0 x:1 x:2 qx:0 w:1:0 w:1:1 u:h:2:1 u:h:0:0 q:h:0:1 u:h:3:0 x:3 u:h:3:1 x:5
+q:h:2:1 u:p:0 x:4 q:h:3:1 u:h:1:0 x:6 q:h:0:0 qx:1 q:h:3:0 u:t:1 u:h:1:1 u:h:2:0 q:p:0 q:h:1:1
+q:h:1:0 q:h:2:0 u:p:1 x:7 u:t:0 L:0 M:0:0 M:0:1 M:0:2 M:0:3 E:0 L:1 M:1:0 M:1:1 M:1:2 L:2 M:1:3
+u:t:3 E:1 M:2:0 M:2:1 M:2:2 M:2:3 L:3 M:3:0 E:2 M:3:1 M:3:2 q:p:1 u:t:2 M:3:3 qx:2 E:3 q:t:1 au:0
+y:0 q:t:0 qx:3
+"""
+PLAN_LATE = """
+y:2 L:4 rc:0 M:4:0 au:1 M:4:1 M:4:2 M:4:3 qy:0 y:1 au:3 E:4 q:t:2 q:t:3 au:2 y:3 qy:1 L:5 rc:3 rc:2
+rc:1 L:6 M:5:0 M:5:1 M:5:2 M:5:3 M:6:0 E:5 M:6:1 M:6:2 L:7 M:6:3 M:7:0 E:6 M:7:1 M:7:2 M:7:3 L:8
+au:5 M:8:0 qy:3 E:7 qy:2 rc:5 M:8:1 au:6 M:8:2 rc:6 M:8:3 E:8 L:9 L:10 M:9:0 M:9:1 M:9:2 au:7 M:9:3
+au:4 rc:7 M:10:0 E:9 M:10:1 M:10:2 L:11 M:10:3 au:8 rc:4 M:11:0 E:10 L:12 M:11:1 M:11:2 M:11:3 rc:8
+M:12:0 M:12:1 E:11 au:9 L:13 M:12:2 au:10 rc:10 M:12:3 M:13:0 E:12 M:13:1 M:13:2 L:14 au:11 M:13:3
+rc:11 rc:9 E:13 M:14:0 M:14:1 M:14:2 au:12 M:14:3 rc:12 L:15 E:14 au:13 M:15:0 M:15:1 M:15:2 M:15:3
+E:15 rc:13 au:14 rc:14 au:15 rc:15
+"""
 
 
 def carry(i):
@@ -54,7 +80,6 @@ def tile_adaptiveinputsoftmax_pa_kernel(tc, x, head_bytes, head_scale, tail_proj
         keep = ctx.enter_context(tc.tile_pool(name="keep", bufs=1))
         work = ctx.enter_context(tc.tile_pool(name="work", bufs=1))
         psum = ctx.enter_context(tc.psum_pool(name="psum", bufs=8))
-        late = {}
 
         ident32 = keep.tile([P, P], F32, name="ident32", align_bytes=64)
         ident16 = keep.tile([P, P], BF16, name="ident16", align_bytes=64)
@@ -72,25 +97,50 @@ def tile_adaptiveinputsoftmax_pa_kernel(tc, x, head_bytes, head_scale, tail_proj
         other = keep.tile([P, TILES], F32, name="other")
         pair = keep.tile([P, TILES, 2], F32, name="pair")
         warm = keep.tile([P, 1], F32, name="warm")
-
         tail_raw = keep.tile([P, 4, TAIL], BF16, name="tail_raw", align_bytes=64)
 
         ctx.enter_context(tc.manual_schedule())
 
-        MODE = {("proj",0):"S",("proj",1):"S",("tail",0):"S"}
-        WIDEN_S = {(h,g,t) for h in range(2) for g in range(2) for t in (2,3)}
+        early = {}
+        late = {}
+        raw = {}
         wide = {}
-        hgrp = {}
+        grouped = {}
         xgrp = {}
-        pgrp = {}
-        wgrp = {}
         ygrp = {}
+        rows = {}
+        state = {}
 
-        def widen(half, g):
+        def load_all():
+            nc.sync.dma_start(out=scale[:], in_=sc_v)
+            hbytes, x_raw, proj_raw = raw["h"], raw["x"], raw["p"]
+
+            def load_bytes(half, g, t0, t1):
+                cols = slice(1024 * half, 1024 * (half + 1))
+                nc.sync.dma_start(out=hbytes[:, g, t0:t1, cols], in_=hb_v[:, g, t0:t1, cols])
+
+            def load_x(i):
+                nc.sync.dma_start(out=x_raw[:, i:i + 2, :], in_=x_v[:, i:i + 2, :])
+
+            load_bytes(0, 0, 0, 2)
+            load_bytes(0, 0, 2, 4)
+            load_bytes(0, 1, 0, 4)
+            load_x(0)
+            load_x(2)
+            load_bytes(1, 0, 0, 4)
+            load_bytes(1, 1, 0, 4)
+            load_x(4)
+            load_x(6)
+            for g in range(2):
+                nc.sync.dma_start(out=proj_raw[:, g, :], in_=pr_v[:, g, :])
+            for d in range(2):
+                nc.sync.dma_start(out=tail_raw[:, :, 1024 * d:1024 * (d + 1)], in_=tw_v[:, :, 1024 * d:1024 * (d + 1)])
+
+        def w(half, g):
             if g == 0:
                 wide[half] = work.tile([P, 2, 4, 1024], BF16, name="wide", tag="row", bufs=4, align_bytes=64)
             for t in range(4):
-                codes = hbytes[:, g, t, 1024 * half:1024 * (half + 1)].bitcast(FP8)
+                codes = raw["h"][:, g, t, 1024 * half:1024 * (half + 1)].bitcast(FP8)
                 if (half, g, t) in WIDEN_S:
                     nc.scalar.activation(out=wide[half][:, g, t, :], in_=codes, func=COPY, scale=scale[:, g, t:t + 1])
                 else:
@@ -98,115 +148,100 @@ def tile_adaptiveinputsoftmax_pa_kernel(tc, x, head_bytes, head_scale, tail_proj
                         out=wide[half][:, g, t, :], in0=codes, scalar1=scale[:, g, t:t + 1], scalar2=None, op0=MULT,
                     )
 
-        def weave(out, planes):
-            for b in range(2):
-                bank = psum.tile([P, 256, 4], BF16, name="bank", tag="bank", bufs=8)
-                for q in range(2):
-                    nc.tensor.matmul(
-                        out=bank[:, 128 * q:128 * (q + 1), :], lhsT=ident16[:], rhs=planes(2 * b + q), start=True, stop=True,
-                    )
-                nc.scalar.copy(
-                    out=out[:, 1024 * b:1024 * (b + 1)].bitcast(F32),
-                    in_=bank[:].rearrange("p n t -> p (n t)").bitcast(F32),
-                )
-
-        def weave_head(c, g):
-            hgrp[c, g] = early.tile([P, 2048], BF16, name="hgrp", tag="hgrp", bufs=4, align_bytes=64)
-            n0 = 512 * (c % 2)
-            if MODE.get(("head", c, g)) != "T":
-                copy = nc.scalar.copy if MODE.get(("head", c, g)) == "S" else nc.vector.tensor_copy
-                copy(
-                    out=hgrp[c, g][:].rearrange("p (c i t) -> p c t i", i=4, t=4),
-                    in_=wide[c // 2][:, g, :, n0:n0 + 512].rearrange("p t (c i) -> p c t i", i=4),
-                )
-                return
-            weave(hgrp[c, g], lambda k: wide[c // 2][:, g, :, n0 + 128 * k:n0 + 128 * (k + 1)].rearrange("p t n -> p n t"))
-
-        def quant_head(c, g):
-            nc.vector.quantize_mx(
-                out=hc[:, g, c * BANK:(c + 1) * BANK].bitcast(FP8X4),
-                scales=hs[:, g, c * BANK:(c + 1) * BANK],
-                in_=hgrp[c, g][:],
-            )
-
-        def turn_x(i):
-            words = x_raw[:, i, :].bitcast(F32)
+        def x_(i):
+            words = raw["x"][:, i, :].bitcast(F32)
             bank = psum.tile([P, 2, 2, P], F32, name="bank", tag="bank", bufs=8)
             for g in range(2):
                 for u in range(2):
                     nc.tensor.transpose(bank[:, g, u, :], words[:, 256 * g + u:256 * (g + 1):2], ident32[:])
-            if i % 2 == 0:
-                xgrp[i // 2] = early.tile([P, 2048], BF16, name="xgrp", tag="xgrp", bufs=3, align_bytes=64)
-            nc.scalar.copy(
+            if i // 2 not in xgrp:
+                xgrp[i // 2] = early["pool"].tile([P, 2048], BF16, name="xgrp", tag="xgrp", bufs=XBUFS, align_bytes=64)
+            copy = nc.vector.tensor_copy if i in X_V else nc.scalar.copy
+            copy(
                 out=xgrp[i // 2][:, 1024 * (i % 2):1024 * (i % 2 + 1)].bitcast(F32).rearrange("p (g r u) -> p g r u", g=2, u=2),
                 in_=bank[:].rearrange("p g u r -> p g r u"),
             )
 
-        def quant_x(k):
+        def qx(k):
             nc.vector.quantize_mx(
                 out=xc[:, 2 * k:2 * k + 2, :].rearrange("p i w -> p (i w)").bitcast(FP8X4),
                 scales=xs[:, 2 * k:2 * k + 2, :].rearrange("p i w -> p (i w)"),
                 in_=xgrp[k][:],
             )
 
-        def weave_proj(g):
-            pgrp[g] = early.tile([P, 2048], BF16, name="pgrp", tag="pgrp", bufs=2, align_bytes=64)
-            view = proj_raw[:, g, :].rearrange("p (j m t) -> p t m j", j=4, t=4)
-            if MODE.get(("proj", g)) != "T":
-                copy = nc.scalar.copy if MODE.get(("proj", g)) == "S" else nc.vector.tensor_copy
-                copy(out=pgrp[g][:].rearrange("p (t m j) -> p t m j", t=4, j=4), in_=view)
-                return
-            weave(pgrp[g], lambda k: view[:, k, :, :])
-
-        def quant_proj(g):
-            nc.vector.quantize_mx(out=pc[:, g, :].bitcast(FP8X4), scales=ps[:, g, :], in_=pgrp[g][:])
-
-        def weave_tail(d):
-            wgrp[d] = work.tile([P, 2048], BF16, name="wgrp", tag="wgrp", bufs=2, align_bytes=64)
-            if MODE.get(("tail", d)) == "T":
-                weave(wgrp[d], lambda k: tail_raw[:, :, 128 * k:128 * (k + 1)].rearrange("p t n -> p n t"))
-                return
-            copy = nc.scalar.copy if MODE.get(("tail", d)) == "S" else nc.vector.tensor_copy
-            copy(
-                out=wgrp[d][:].rearrange("p (c i t) -> p c t i", i=4, t=4),
-                in_=tail_raw[:, :, BANK * d:BANK * (d + 1)].rearrange("p t (c i) -> p c t i", i=4),
-            )
-
-        def quant_tail(d):
-            nc.vector.quantize_mx(
-                out=wc[:, BANK * d:BANK * (d + 1)].bitcast(FP8X4),
-                scales=ws[:, BANK * d:BANK * (d + 1)],
-                in_=wgrp[d][:],
-            )
-
-        def make_y(i):
-            bank = psum.tile([P, 4, P], F32, name="bank", tag="bank", bufs=8)
-            for t in range(4):
-                for g in range(2):
-                    nc.tensor.matmul_mx(
-                        out=bank[:, t, :],
-                        lhsT=pc[:, g, P * t:P * (t + 1)].bitcast(FP8X4),
-                        lhsT_scale=ps[:, g, P * t:P * (t + 1)],
-                        rhs=xc[:, i, P * g:P * (g + 1)].bitcast(FP8X4),
-                        rhs_scale=xs[:, i, P * g:P * (g + 1)],
-                        start=(g == 0),
-                        stop=(g == 1),
+        def u(kind, a, g=0):
+            pool, bufs = (work, 4) if kind == "t" else (early["pool"], 2 if kind == "p" else HBUFS)
+            out = pool.tile([P, 2048], BF16, name="grp_" + kind, tag="grp_" + kind, bufs=bufs, align_bytes=64)
+            key = (kind, a, g) if kind == "h" else (kind, a)
+            grouped[key] = out
+            mode = UNITS[key]
+            if kind == "p":
+                src = raw["p"][:, a, :].rearrange("p (j m t) -> p t m j", j=4, t=4)
+                dst = out[:].rearrange("p (t m j) -> p t m j", t=4, j=4)
+                part = lambda k: src[:, k, :, :]
+            else:
+                if kind == "h":
+                    n0 = BANK * (a % 2)
+                    planes = wide[a // 2][:, g, :, n0:n0 + BANK]
+                else:
+                    planes = tail_raw[:, :, BANK * a:BANK * (a + 1)]
+                src = planes.rearrange("p t (c i) -> p c t i", i=4)
+                dst = out[:].rearrange("p (c i t) -> p c t i", i=4, t=4)
+                part = lambda k: planes[:, :, 128 * k:128 * (k + 1)].rearrange("p t n -> p n t")
+            if mode == "T":
+                for b in range(2):
+                    bank = psum.tile([P, 256, 4], BF16, name="bank", tag="bank", bufs=8)
+                    for q in range(2):
+                        nc.tensor.matmul(
+                            out=bank[:, 128 * q:128 * (q + 1), :], lhsT=ident16[:], rhs=part(2 * b + q), start=True, stop=True,
+                        )
+                    nc.scalar.copy(
+                        out=out[:, 1024 * b:1024 * (b + 1)].bitcast(F32),
+                        in_=bank[:].rearrange("p n t -> p (n t)").bitcast(F32),
                     )
-            if i % 2 == 0:
-                ygrp[i // 2] = work.tile([P, 2, P, 4], BF16, name="ygrp", tag="ygrp", bufs=2, align_bytes=64)
-            nc.scalar.copy(out=ygrp[i // 2][:, i % 2], in_=bank[:].rearrange("p t n -> p n t"))
+            elif mode == "G":
+                nc.gpsimd.tensor_scalar(out=dst, in0=src, scalar1=1.0, scalar2=0.0, op0=MULT, op1=ADD)
+            elif mode == "S":
+                nc.scalar.copy(out=dst, in_=src)
+            else:
+                nc.vector.tensor_copy(out=dst, in_=src)
 
-        def quant_y(k):
+        def q(kind, a, g=0):
+            if kind == "h":
+                codes, scales, key = hc[:, g, a * BANK:(a + 1) * BANK], hs[:, g, a * BANK:(a + 1) * BANK], (kind, a, g)
+            elif kind == "p":
+                codes, scales, key = pc[:, a, :], ps[:, a, :], (kind, a)
+            else:
+                codes, scales, key = wc[:, BANK * a:BANK * (a + 1)], ws[:, BANK * a:BANK * (a + 1)], (kind, a)
+            nc.vector.quantize_mx(out=codes.bitcast(FP8X4), scales=scales, in_=grouped[key][:])
+
+        def y(k):
+            ygrp[k] = work.tile([P, 2, P, 4], BF16, name="ygrp", tag="ygrp", bufs=4, align_bytes=64)
+            for i in (2 * k, 2 * k + 1):
+                bank = psum.tile([P, 4, P], F32, name="bank", tag="bank", bufs=8)
+                for t in range(4):
+                    for g in range(2):
+                        nc.tensor.matmul_mx(
+                            out=bank[:, t, :],
+                            lhsT=pc[:, g, P * t:P * (t + 1)].bitcast(FP8X4),
+                            lhsT_scale=ps[:, g, P * t:P * (t + 1)],
+                            rhs=xc[:, i, P * g:P * (g + 1)].bitcast(FP8X4),
+                            rhs_scale=xs[:, i, P * g:P * (g + 1)],
+                            start=(g == 0),
+                            stop=(g == 1),
+                        )
+                copy = nc.vector.tensor_copy if i in Y_V else nc.scalar.copy
+                copy(out=ygrp[k][:, i % 2], in_=bank[:].rearrange("p t n -> p n t"))
+
+        def qy(k):
             nc.vector.quantize_mx(
                 out=yc[:, 2 * k:2 * k + 2, :].rearrange("p i n -> p (i n)").bitcast(FP8X4),
                 scales=ys[:, 2 * k:2 * k + 2, :].rearrange("p i n -> p (i n)"),
                 in_=ygrp[k][:].rearrange("p i n t -> p (i n t)"),
             )
 
-        rows = {}
-        state = {}
-
-        def logits(kind, i):
+        def L(n):
+            kind, i = SEQ[n]
             banks = []
             for c in range(4):
                 bank = psum.tile([P, BANK], F32, name="bank", tag="bank", bufs=8)
@@ -233,197 +268,92 @@ def tile_adaptiveinputsoftmax_pa_kernel(tc, x, head_bytes, head_scale, tail_proj
                         stop=True,
                     )
                 banks.append(bank)
-            return banks
+            state[n] = {"banks": banks}
 
-        def add_up(group):
-            sums = state[group[0]]["sums"]
-            k0 = state[group[0]]["slot"]
-            total = work.tile([P, 2], F32, name="total", tag="total", bufs=4)
-            m = len(group)
-            nc.vector.tensor_reduce(out=total[:, 0:m], in_=sums[:, k0:k0 + m, :], axis=AX, op=ADD)
-            state["total", group[0]] = total
+        def M(n, c):
+            st = state[n]
+            if c == 0:
+                st["peaks"] = work.tile([P, 4], F32, name="peaks", tag="peaks", bufs=4)
+            nc.vector.tensor_reduce(out=st["peaks"][:, c:c + 1], in_=st["banks"][c][:], axis=AX, op=MAX)
 
-        def finish(group):
-            m = len(group)
-            inv = work.tile([P, 2], F32, name="inv", tag="inv", bufs=6)
-            nc.vector.reciprocal(out=inv[:, 0:m], in_=state["total", group[0]][:, 0:m])
-            for k, (kind, i) in enumerate(group):
-                scale_out(kind, i, inv[:, k:k + 1])
-
-        def scale_out(kind, i, inv):
-            row, c0 = rows[i], carry(i)
-            last = i == TILES - 1
-            split = down8(c0 + TOKENS_OUT)
-            if kind == "h":
-                engine = nc.vector if ("h", i) in ON_VECTOR else nc.gpsimd
-                engine.tensor_scalar(out=row[:, c0:c0 + TOKENS_OUT], in0=row[:, c0:c0 + TOKENS_OUT], scalar1=inv, scalar2=0.0, op0=MULT, op1=ADD)
-                clus = state[kind, i]["clus"]
-                nc.gpsimd.tensor_scalar(out=pair[:, i, :], in0=clus[:], scalar1=inv, scalar2=0.0, op0=MULT, op1=ADD)
-                nc.sync.dma_start(out=out_v[:, ROW * i - c0 + up8(c0):ROW * i - c0 + split], in_=row[:, up8(c0):split])
-                if last:
-                    nc.gpsimd.tensor_copy(out=other[:], in_=pair[:, :, 1])
-                    nc.sync.dma_start(out=out1_v, in_=other[:])
-            else:
-                prob = pair[:, i, 0:1]
-                base = c0 + TOKENS_OUT
-                end = c0 + ROW
-                if not last:
-                    engine = nc.vector if ("t", i) in ON_VECTOR else nc.gpsimd
-                    engine.tensor_scalar(
-                        out=row[:, base:end], in0=row[:, base:end], scalar1=inv, scalar2=prob, op0=MULT, op1=MULT,
-                    )
-                    if up8(end) > end:
-                        c1 = carry(i + 1)
-                        engine.tensor_copy(out=row[:, end:up8(end)], in_=rows[i + 1][:, c1:8])
-                    nc.sync.dma_start(out=out_v[:, ROW * i - c0 + split:ROW * i - c0 + up8(end)], in_=row[:, split:up8(end)])
-                else:
-                    for a in range(0, TAIL, 512):
-                        nc.vector.tensor_scalar(
-                            out=row[:, base + a:base + a + 512], in0=row[:, base + a:base + a + 512],
-                            scalar1=inv, scalar2=prob, op0=MULT, op1=MULT,
-                        )
-                        nc.sync.dma_start(out=out_v[:, ROW * i + TOKENS_OUT + a:ROW * i + TOKENS_OUT + a + 512], in_=row[:, base + a:base + a + 512])
-
-        SEQ = [("h", 0), ("h", 1), ("h", 2), ("h", 3), ("t", 0), ("h", 4), ("t", 1), ("h", 5), ("t", 2), ("h", 6), ("t", 3), ("h", 7), ("t", 4), ("t", 5), ("t", 6), ("t", 7)]
-
-        ON_VECTOR = {("h", 0), ("t", 5), ("t", 6)}
-        GROUPS = {4: SEQ[2:3], 5: SEQ[3:4], 7: SEQ[4:6], 9: SEQ[6:8], 11: SEQ[8:10], 13: SEQ[10:12], 15: SEQ[12:13]}
-
-        def peaks(n, then=()):
+        def E(n):
             kind, i = SEQ[n]
-            st = {}
-            state[kind, i] = st
-            st["banks"] = logits(kind, i)
-            st["peaks"] = work.tile([P, 4], F32, name="peaks", tag="peaks", bufs=4)
-            for c in range(4):
-                nc.vector.tensor_reduce(out=st["peaks"][:, c:c + 1], in_=st["banks"][c][:], axis=AX, op=mybir.AluOpType.max)
-                if c < len(then):
-                    then[c]()
-
-        def exps(n):
-            kind, i = SEQ[n]
-            st = state[kind, i]
+            st = state[n]
             if kind == "h":
                 if 4 <= i < 7:
                     rows[i] = late["pool"].tile([P, 4104], F32, name="late_row", tag="late_row", bufs=3, align_bytes=64)
                 else:
                     rows[i] = work.tile([P, 4104], F32, name="row", tag="row", bufs=4, align_bytes=64)
             negmax = work.tile([P, 1], F32, name="negmax", tag="negmax", bufs=4)
-            nc.vector.tensor_reduce(out=negmax[:], in_=st["peaks"][:], axis=AX, op=mybir.AluOpType.max, negate=True)
-            if n % 2 == 0:
-                st["sums"] = work.tile([P, 2, 4], F32, name="sums4", tag="sums4", bufs=4)
-            else:
-                st["sums"] = state[SEQ[n - 1]]["sums"]
-            st["slot"] = n % 2
+            nc.vector.tensor_reduce(out=negmax[:], in_=st["peaks"][:], axis=AX, op=MAX, negate=True)
+            st["sums"] = work.tile([P, 4], F32, name="sums4", tag="sums4", bufs=8)
             start = carry(i) + (0 if kind == "h" else TOKENS_OUT)
             for c in range(4):
                 nc.scalar.activation(
                     out=rows[i][:, start + BANK * c:start + BANK * (c + 1)], in_=st["banks"][c][:], func=EXP,
-                    bias=negmax[:], scale=1.0, accum_out=st["sums"][:, st["slot"], c:c + 1],
+                    bias=negmax[:], scale=1.0, accum_out=st["sums"][:, c:c + 1],
                 )
             if kind == "h":
-                st["clus"] = work.tile([P, 2], F32, name="clus", tag="clus", bufs=5)
+                st["clus"] = work.tile([P, 2], F32, name="clus", tag="clus", bufs=8)
                 nc.scalar.copy(out=st["clus"][:], in_=rows[i][:, start + TOKENS_OUT:start + HEAD])
 
-        with tc.tile_pool(name="early", bufs=1) as early:
-            hbytes = early.tile([P, 2, 4, HEAD], U8, name="hbytes", align_bytes=64)
-            proj_raw = early.tile([P, 2, 4 * H], BF16, name="proj_raw", align_bytes=64)
-            x_raw = early.tile([P, TILES, D_IN], BF16, name="x_raw", align_bytes=64)
-            nc.sync.dma_start(out=scale[:], in_=sc_v)
-            for half in range(2):
-                for g in range(2):
-                    cols = slice(1024 * half, 1024 * (half + 1))
-                    if half == 0 and g == 0:
-                        nc.sync.dma_start(out=hbytes[:, g, 0:2, cols], in_=hb_v[:, g, 0:2, cols])
-                        nc.sync.dma_start(out=hbytes[:, g, 2:4, cols], in_=hb_v[:, g, 2:4, cols])
-                    else:
-                        nc.sync.dma_start(out=hbytes[:, g, :, cols], in_=hb_v[:, g, :, cols])
-                    i = 4 * half + 2 * g
-                    nc.sync.dma_start(out=x_raw[:, i:i + 2, :], in_=x_v[:, i:i + 2, :])
-            for g in range(2):
-                nc.sync.dma_start(out=proj_raw[:, g, :], in_=pr_v[:, g, :])
-            for d in range(2):
-                nc.sync.dma_start(out=tail_raw[:, :, 1024 * d:1024 * (d + 1)], in_=tw_v[:, :, 1024 * d:1024 * (d + 1)])
+        def au(n):
+            total = work.tile([P, 1], F32, name="total", tag="total", bufs=8)
+            nc.vector.tensor_reduce(out=total[:], in_=state[n]["sums"][:], axis=AX, op=ADD)
+            state[n]["total"] = total
 
+        def rc(n):
+            kind, i = SEQ[n]
+            inv_t = work.tile([P, 1], F32, name="inv", tag="inv", bufs=8)
+            inv = inv_t[:]
+            nc.vector.reciprocal(out=inv, in_=state[n]["total"][:])
+            row, c0 = rows[i], carry(i)
+            split = down8(c0 + TOKENS_OUT)
+            engine = nc.vector if SEQ[n] in ON_VECTOR else nc.gpsimd
+            if kind == "h":
+                engine.tensor_scalar(out=row[:, c0:c0 + TOKENS_OUT], in0=row[:, c0:c0 + TOKENS_OUT], scalar1=inv, scalar2=0.0, op0=MULT, op1=ADD)
+                nc.gpsimd.tensor_scalar(out=pair[:, i, :], in0=state[n]["clus"][:], scalar1=inv, scalar2=0.0, op0=MULT, op1=ADD)
+                nc.sync.dma_start(out=out_v[:, ROW * i - c0 + up8(c0):ROW * i - c0 + split], in_=row[:, up8(c0):split])
+                if i == TILES - 1:
+                    nc.gpsimd.tensor_copy(out=other[:], in_=pair[:, :, 1])
+                    nc.sync.dma_start(out=out1_v, in_=other[:])
+            else:
+                prob = pair[:, i, 0:1]
+                base = c0 + TOKENS_OUT
+                end = c0 + ROW
+                if i < TILES - 1:
+                    if up8(end) > end:
+                        c1 = carry(i + 1)
+                        engine.tensor_copy(out=row[:, end:up8(end)], in_=rows[i + 1][:, c1:8])
+                    engine.tensor_scalar(out=row[:, base:end], in0=row[:, base:end], scalar1=inv, scalar2=prob, op0=MULT, op1=MULT)
+                    nc.sync.dma_start(out=out_v[:, ROW * i - c0 + split:ROW * i - c0 + up8(end)], in_=row[:, split:up8(end)])
+                else:
+                    for a in range(0, TAIL, 512):
+                        engine.tensor_scalar(
+                            out=row[:, base + a:base + a + 512], in0=row[:, base + a:base + a + 512],
+                            scalar1=inv, scalar2=prob, op0=MULT, op1=MULT,
+                        )
+                        nc.sync.dma_start(out=out_v[:, ROW * i + TOKENS_OUT + a:ROW * i + TOKENS_OUT + a + 512], in_=row[:, base + a:base + a + 512])
+
+        STEPS = {"w": w, "x": x_, "qx": qx, "u": u, "q": q, "y": y, "qy": qy, "L": L, "M": M, "E": E, "au": au, "rc": rc}
+
+        def go(plan):
+            for step in plan.split():
+                parts = step.split(":")
+                args = [int(a) if a not in "hpt" else a for a in parts[1:]]
+                STEPS[parts[0]](*args)
+
+        with tc.tile_pool(name="early", bufs=1) as early_pool:
+            early["pool"] = early_pool
+            raw_h = early_pool.tile([P, 2, 4, HEAD], U8, name="hbytes", align_bytes=64)
+            raw_p = early_pool.tile([P, 2, 4 * H], BF16, name="proj_raw", align_bytes=64)
+            raw_x = early_pool.tile([P, TILES, D_IN], BF16, name="x_raw", align_bytes=64)
+            raw["h"], raw["p"], raw["x"] = raw_h, raw_p, raw_x
+            load_all()
             nc.vector.memset(warm[:], 0.0)
             nc.scalar.activation(out=warm[:], in_=warm[:], func=EXP)
             make_identity(nc, ident32[:])
             make_identity(nc, ident16[:])
-
-            widen(0, 0)
-            turn_x(0)
-            turn_x(1)
-            weave_head(0, 0)
-            weave_head(1, 0)
-            widen(0, 1)
-            quant_x(0)
-            turn_x(2)
-            turn_x(3)
-            weave_head(0, 1)
-            weave_head(1, 1)
-            quant_head(0, 0)
-            quant_head(1, 0)
-            widen(1, 0)
-            quant_x(1)
-            turn_x(4)
-            turn_x(5)
-            weave_head(2, 0)
-            weave_head(3, 0)
-            quant_head(0, 1)
-            quant_head(1, 1)
-            widen(1, 1)
-            quant_x(2)
-            turn_x(6)
-            turn_x(7)
-            weave_proj(0)
-            weave_head(2, 1)
-            weave_head(3, 1)
-            weave_proj(1)
-            quant_head(2, 0)
-            quant_head(3, 0)
-            quant_x(3)
-            quant_proj(0)
-            weave_tail(0)
-            quant_head(2, 1)
-            quant_head(3, 1)
-            quant_proj(1)
+            go(PLAN_EARLY)
         late["pool"] = ctx.enter_context(tc.tile_pool(name="late", bufs=1))
-        peaks(0)
-        peaks(1, [lambda: exps(0)])
-        for i in range(4):
-            make_y(i)
-        weave_tail(1)
-        exps(1)
-        quant_tail(0)
-        weave_tail(2)
-        add_up(SEQ[0:1])
-        quant_tail(1)
-        finish(SEQ[0:1])
-        weave_tail(3)
-        quant_tail(2)
-        for i in range(4, 8):
-            make_y(i)
-        quant_y(0)
-        add_up(SEQ[1:2])
-        quant_tail(3)
-        finish(SEQ[1:2])
-        peaks(2)
-        quant_y(1)
-        exps(2)
-        quant_y(2)
-        quant_y(3)
-        for n in range(3, 16):
-            group = GROUPS.get(n)
-            then = []
-            if n > 3:
-                then.append(lambda: exps(n - 1))
-            if group:
-                then += [lambda: add_up(group), lambda: finish(group)]
-            peaks(n, then)
-        exps(15)
-        add_up(SEQ[13:14])
-        finish(SEQ[13:14])
-        add_up(SEQ[14:15])
-        finish(SEQ[14:15])
-        add_up(SEQ[15:16])
-        finish(SEQ[15:16])
+        go(PLAN_LATE)

@@ -28,29 +28,31 @@ BANK = 512
 
 FLOPS = 2 * 1024 * (D_IN * HEAD + D_IN * H + H * TAIL)
 
-SEQ = [('h', 0), ('h', 1), ('h', 2), ('h', 3), ('h', 4), ('t', 0), ('h', 5), ('t', 1), ('h', 6), ('t', 2), ('h', 7), ('t', 3), ('t', 4), ('t', 5), ('t', 6), ('t', 7)]
-UNITS = {('h', 0, 0): 'T', ('h', 0, 1): 'V', ('h', 1, 0): 'T', ('h', 1, 1): 'V', ('h', 2, 0): 'V', ('h', 2, 1): 'S', ('h', 3, 0): 'V', ('h', 3, 1): 'V', ('p', 0): 'T', ('p', 1): 'G', ('t', 0): 'T', ('t', 1): 'S', ('t', 2): 'G', ('t', 3): 'G'}
-WIDEN_S = {(1, 0, 1), (1, 1, 0), (0, 0, 2), (0, 1, 2), (1, 0, 2)}
-ON_VECTOR = {('t', 3), ('t', 5), ('t', 6), ('t', 7)}
+LOADS = ['b00a', 'b00b', 'b10', 'x1', 'b11', 'b01', 'x3', 'p1', 'p0', 'x0', 't0', 'x2', 't1']
+ON_SCALAR = {('h', 0), ('h', 7)}
+SEQ = [('h', 0), ('h', 1), ('h', 2), ('h', 3), ('t', 0), ('h', 4), ('t', 1), ('h', 5), ('t', 2), ('h', 6), ('t', 3), ('h', 7), ('t', 4), ('t', 5), ('t', 6), ('t', 7)]
+UNITS = {('h', 0, 0): 'T', ('h', 0, 1): 'T', ('h', 1, 0): 'V', ('h', 1, 1): 'V', ('h', 2, 0): 'V', ('h', 2, 1): 'T', ('h', 3, 0): 'V', ('h', 3, 1): 'T', ('p', 0): 'V', ('p', 1): 'S', ('t', 0): 'G', ('t', 1): 'S', ('t', 2): 'G', ('t', 3): 'G'}
+WIDEN_S = {(1, 0, 1), (1, 1, 0), (0, 0, 3), (0, 1, 3), (1, 0, 0), (0, 1, 2)}
+ON_VECTOR = {('t', 5), ('t', 6), ('t', 7), ('t', 4)}
 X_V = ()
-Y_V = {1}
+Y_V = {5, 6}
 HBUFS = 4
 XBUFS = 3
 PLAN_EARLY = """
-w:0:0 w:0:1 u:h:0:1 x:0 x:1 x:2 qx:0 w:1:0 w:1:1 u:h:2:1 u:h:0:0 q:h:0:1 u:h:3:0 x:3 u:h:3:1 x:5
-q:h:2:1 u:p:0 x:4 q:h:3:1 u:h:1:0 x:6 q:h:0:0 qx:1 q:h:3:0 u:t:1 u:h:1:1 u:h:2:0 q:p:0 q:h:1:1
-q:h:1:0 q:h:2:0 u:p:1 x:7 u:t:0 L:0 M:0:0 M:0:1 M:0:2 M:0:3 E:0 L:1 M:1:0 M:1:1 M:1:2 L:2 M:1:3
-u:t:3 E:1 M:2:0 M:2:1 M:2:2 M:2:3 L:3 M:3:0 E:2 M:3:1 M:3:2 q:p:1 u:t:2 M:3:3 qx:2 E:3 q:t:1 au:0
-y:0 q:t:0 qx:3
+w:0:0 u:t:2 w:1:0 u:h:1:0 w:1:1 u:h:0:0 w:0:1 q:h:0:0 u:p:1 u:h:2:0 q:h:1:0 x:3 x:2 u:h:3:0 u:h:3:1
+u:p:0 u:h:0:1 x:1 q:h:2:0 q:h:3:0 u:h:2:1 qx:1 q:p:0 q:p:1 x:5 x:0 x:4 u:h:1:1 x:6 q:h:2:1 q:h:1:1
+qx:0 q:h:0:1 qx:2 y:1 q:h:3:1 qy:1 x:7 L:0 u:t:1 M:0:0 M:0:1 L:1 M:0:2 M:0:3 M:1:0 E:0 M:1:1 u:t:3
+M:1:2 L:2 M:1:3 M:2:0 E:1 L:3 M:2:1 M:2:2 M:2:3 M:3:0 E:2 M:3:1 y:0 au:0 u:t:0 au:1 M:3:2 M:3:3
+q:t:3 qx:3
 """
 PLAN_LATE = """
-y:2 L:4 rc:0 M:4:0 au:1 M:4:1 M:4:2 M:4:3 qy:0 y:1 au:3 E:4 q:t:2 q:t:3 au:2 y:3 qy:1 L:5 rc:3 rc:2
-rc:1 L:6 M:5:0 M:5:1 M:5:2 M:5:3 M:6:0 E:5 M:6:1 M:6:2 L:7 M:6:3 M:7:0 E:6 M:7:1 M:7:2 M:7:3 L:8
-au:5 M:8:0 qy:3 E:7 qy:2 rc:5 M:8:1 au:6 M:8:2 rc:6 M:8:3 E:8 L:9 L:10 M:9:0 M:9:1 M:9:2 au:7 M:9:3
-au:4 rc:7 M:10:0 E:9 M:10:1 M:10:2 L:11 M:10:3 au:8 rc:4 M:11:0 E:10 L:12 M:11:1 M:11:2 M:11:3 rc:8
-M:12:0 M:12:1 E:11 au:9 L:13 M:12:2 au:10 rc:10 M:12:3 M:13:0 E:12 M:13:1 M:13:2 L:14 au:11 M:13:3
-rc:11 rc:9 E:13 M:14:0 M:14:1 M:14:2 au:12 M:14:3 rc:12 L:15 E:14 au:13 M:15:0 M:15:1 M:15:2 M:15:3
-E:15 rc:13 au:14 rc:14 au:15 rc:15
+q:t:0 E:3 q:t:1 rc:1 q:t:2 qy:0 y:2 rc:0 y:3 L:4 au:2 M:4:0 au:3 rc:2 M:4:1 rc:3 L:5 qy:2 M:4:2
+M:4:3 M:5:0 E:4 M:5:1 M:5:2 L:6 M:5:3 M:6:0 E:5 M:6:1 au:4 M:6:2 rc:4 qy:3 M:6:3 L:7 M:7:0 E:6 M:7:1
+au:5 M:7:2 rc:5 M:7:3 L:8 M:8:0 E:7 M:8:1 au:6 M:8:2 rc:6 M:8:3 L:9 M:9:0 E:8 M:9:1 au:7 M:9:2 rc:7
+M:9:3 L:10 M:10:0 E:9 M:10:1 au:8 M:10:2 rc:8 M:10:3 L:11 M:11:0 E:10 M:11:1 au:9 M:11:2 rc:9 M:11:3
+L:12 M:12:0 E:11 M:12:1 au:10 M:12:2 rc:10 M:12:3 L:13 M:13:0 E:12 M:13:1 au:11 M:13:2 rc:11 M:13:3
+L:14 M:14:0 E:13 M:14:1 au:12 M:14:2 rc:12 M:14:3 L:15 M:15:0 E:14 M:15:1 au:13 M:15:2 rc:13 M:15:3
+E:15 au:14 rc:14 au:15 rc:15
 """
 
 
@@ -122,19 +124,19 @@ def tile_adaptiveinputsoftmax_pa_kernel(tc, x, head_bytes, head_scale, tail_proj
             def load_x(i):
                 nc.sync.dma_start(out=x_raw[:, i:i + 2, :], in_=x_v[:, i:i + 2, :])
 
-            load_bytes(0, 0, 0, 2)
-            load_bytes(0, 0, 2, 4)
-            load_bytes(0, 1, 0, 4)
-            load_x(0)
-            load_x(2)
-            load_bytes(1, 0, 0, 4)
-            load_bytes(1, 1, 0, 4)
-            load_x(4)
-            load_x(6)
-            for g in range(2):
-                nc.sync.dma_start(out=proj_raw[:, g, :], in_=pr_v[:, g, :])
-            for d in range(2):
-                nc.sync.dma_start(out=tail_raw[:, :, 1024 * d:1024 * (d + 1)], in_=tw_v[:, :, 1024 * d:1024 * (d + 1)])
+            for name in LOADS:
+                if name[0] == "b":
+                    half, g = int(name[1]), int(name[2])
+                    t0, t1 = {"a": (0, 2), "b": (2, 4), "": (0, 4)}[name[3:]]
+                    load_bytes(half, g, t0, t1)
+                elif name[0] == "x":
+                    load_x(2 * int(name[1]))
+                elif name[0] == "p":
+                    g = int(name[1])
+                    nc.sync.dma_start(out=proj_raw[:, g, :], in_=pr_v[:, g, :])
+                else:
+                    cols = slice(1024 * int(name[1]), 1024 * (int(name[1]) + 1))
+                    nc.sync.dma_start(out=tail_raw[:, :, cols], in_=tw_v[:, :, cols])
 
         def w(half, g):
             if g == 0:
@@ -280,8 +282,8 @@ def tile_adaptiveinputsoftmax_pa_kernel(tc, x, head_bytes, head_scale, tail_proj
             kind, i = SEQ[n]
             st = state[n]
             if kind == "h":
-                if 4 <= i < 7:
-                    rows[i] = late["pool"].tile([P, 4104], F32, name="late_row", tag="late_row", bufs=3, align_bytes=64)
+                if i >= 4:
+                    rows[i] = late["pool"].tile([P, 4104], F32, name="late_row", tag="late_row", bufs=4, align_bytes=64)
                 else:
                     rows[i] = work.tile([P, 4104], F32, name="row", tag="row", bufs=4, align_bytes=64)
             negmax = work.tile([P, 1], F32, name="negmax", tag="negmax", bufs=4)
@@ -309,10 +311,31 @@ def tile_adaptiveinputsoftmax_pa_kernel(tc, x, head_bytes, head_scale, tail_proj
             nc.vector.reciprocal(out=inv, in_=state[n]["total"][:])
             row, c0 = rows[i], carry(i)
             split = down8(c0 + TOKENS_OUT)
-            engine = nc.vector if SEQ[n] in ON_VECTOR else nc.gpsimd
+            if SEQ[n] in ON_SCALAR:
+                move = nc.scalar.copy
+
+                def scaled(out, by):
+                    if len(by) == 1:
+                        nc.scalar.activation(out=out, in_=out, func=COPY, scale=by[0])
+                    else:
+                        both = work.tile([P, 1], F32, name="both", tag="both", bufs=4)
+                        nc.scalar.activation(out=both[:], in_=by[0], func=COPY, scale=by[1])
+                        nc.scalar.activation(out=out, in_=out, func=COPY, scale=both[:])
+            else:
+                engine = nc.vector if SEQ[n] in ON_VECTOR else nc.gpsimd
+                move = engine.tensor_copy
+
+                def scaled(out, by):
+                    if len(by) == 1:
+                        engine.tensor_scalar(out=out, in0=out, scalar1=by[0], scalar2=0.0, op0=MULT, op1=ADD)
+                    else:
+                        engine.tensor_scalar(out=out, in0=out, scalar1=by[0], scalar2=by[1], op0=MULT, op1=MULT)
             if kind == "h":
-                engine.tensor_scalar(out=row[:, c0:c0 + TOKENS_OUT], in0=row[:, c0:c0 + TOKENS_OUT], scalar1=inv, scalar2=0.0, op0=MULT, op1=ADD)
-                nc.gpsimd.tensor_scalar(out=pair[:, i, :], in0=state[n]["clus"][:], scalar1=inv, scalar2=0.0, op0=MULT, op1=ADD)
+                if SEQ[n] in ON_SCALAR:
+                    nc.scalar.activation(out=pair[:, i, :], in_=state[n]["clus"][:], func=COPY, scale=inv)
+                else:
+                    engine.tensor_scalar(out=pair[:, i, :], in0=state[n]["clus"][:], scalar1=inv, scalar2=0.0, op0=MULT, op1=ADD)
+                scaled(row[:, c0:c0 + TOKENS_OUT], [inv])
                 nc.sync.dma_start(out=out_v[:, ROW * i - c0 + up8(c0):ROW * i - c0 + split], in_=row[:, up8(c0):split])
                 if i == TILES - 1:
                     nc.gpsimd.tensor_copy(out=other[:], in_=pair[:, :, 1])
@@ -324,15 +347,12 @@ def tile_adaptiveinputsoftmax_pa_kernel(tc, x, head_bytes, head_scale, tail_proj
                 if i < TILES - 1:
                     if up8(end) > end:
                         c1 = carry(i + 1)
-                        engine.tensor_copy(out=row[:, end:up8(end)], in_=rows[i + 1][:, c1:8])
-                    engine.tensor_scalar(out=row[:, base:end], in0=row[:, base:end], scalar1=inv, scalar2=prob, op0=MULT, op1=MULT)
+                        move(out=row[:, end:up8(end)], in_=rows[i + 1][:, c1:8])
+                    scaled(row[:, base:end], [inv, prob])
                     nc.sync.dma_start(out=out_v[:, ROW * i - c0 + split:ROW * i - c0 + up8(end)], in_=row[:, split:up8(end)])
                 else:
                     for a in range(0, TAIL, 512):
-                        engine.tensor_scalar(
-                            out=row[:, base + a:base + a + 512], in0=row[:, base + a:base + a + 512],
-                            scalar1=inv, scalar2=prob, op0=MULT, op1=MULT,
-                        )
+                        scaled(row[:, base + a:base + a + 512], [inv, prob])
                         nc.sync.dma_start(out=out_v[:, ROW * i + TOKENS_OUT + a:ROW * i + TOKENS_OUT + a + 512], in_=row[:, base + a:base + a + 512])
 
         STEPS = {"w": w, "x": x_, "qx": qx, "u": u, "q": q, "y": y, "qy": qy, "L": L, "M": M, "E": E, "au": au, "rc": rc}

from contextlib import ExitStack

import concourse.mybir as mybir
from concourse.masks import make_identity

F32 = mybir.dt.float32
BF16 = mybir.dt.bfloat16
U32 = mybir.dt.uint32
U8 = mybir.dt.uint8
FP8 = mybir.dt.float8_e4m3fn
FP8X4 = mybir.dt.float8_e4m3fn_x4
EXP = mybir.ActivationFunctionType.Exp
COPY = mybir.ActivationFunctionType.Copy
MULT = mybir.AluOpType.mult
ADD = mybir.AluOpType.add
MAX = mybir.AluOpType.max
AX = mybir.AxisListType.X

P = 128
TILES = 8
D_IN = 1024
HEAD = 2048
TOKENS_OUT = 2046
H = 512
TAIL = 2048
ROW = 4094
BANK = 512

FLOPS = 2 * 1024 * (D_IN * HEAD + D_IN * H + H * TAIL)

LOADS = ['b00a', 'b00b', 'b10', 'x1', 'b11', 'b01', 'x3', 'p1', 'p0', 'x0', 't0', 'x2', 't1']
ON_SCALAR = {('h', 0), ('h', 7)}
SEQ = [('h', 0), ('h', 1), ('h', 2), ('h', 3), ('t', 0), ('h', 4), ('t', 1), ('h', 5), ('t', 2), ('h', 6), ('t', 3), ('h', 7), ('t', 4), ('t', 5), ('t', 6), ('t', 7)]
UNITS = {('h', 0, 0): 'T', ('h', 0, 1): 'T', ('h', 1, 0): 'V', ('h', 1, 1): 'V', ('h', 2, 0): 'V', ('h', 2, 1): 'T', ('h', 3, 0): 'V', ('h', 3, 1): 'T', ('p', 0): 'V', ('p', 1): 'S', ('t', 0): 'G', ('t', 1): 'S', ('t', 2): 'G', ('t', 3): 'G'}
WIDEN_S = {(1, 0, 1), (1, 1, 0), (0, 0, 3), (0, 1, 3), (1, 0, 0), (0, 1, 2)}
ON_VECTOR = {('t', 5), ('t', 6), ('t', 7), ('t', 4)}
X_V = ()
Y_V = {5, 6}
HBUFS = 4
XBUFS = 3
PLAN_EARLY = """
w:0:0 u:t:2 w:1:0 u:h:1:0 w:1:1 u:h:0:0 w:0:1 q:h:0:0 u:p:1 u:h:2:0 q:h:1:0 x:3 x:2 u:h:3:0 u:h:3:1
u:p:0 u:h:0:1 x:1 q:h:2:0 q:h:3:0 u:h:2:1 qx:1 q:p:0 q:p:1 x:5 x:0 x:4 u:h:1:1 x:6 q:h:2:1 q:h:1:1
qx:0 q:h:0:1 qx:2 y:1 q:h:3:1 qy:1 x:7 L:0 u:t:1 M:0:0 M:0:1 L:1 M:0:2 M:0:3 M:1:0 E:0 M:1:1 u:t:3
M:1:2 L:2 M:1:3 M:2:0 E:1 L:3 M:2:1 M:2:2 M:2:3 M:3:0 E:2 M:3:1 y:0 au:0 u:t:0 au:1 M:3:2 M:3:3
q:t:3 qx:3
"""
PLAN_LATE = """
q:t:0 E:3 q:t:1 rc:1 q:t:2 qy:0 y:2 rc:0 y:3 L:4 au:2 M:4:0 au:3 rc:2 M:4:1 rc:3 L:5 qy:2 M:4:2
M:4:3 M:5:0 E:4 M:5:1 M:5:2 L:6 M:5:3 M:6:0 E:5 M:6:1 au:4 M:6:2 rc:4 qy:3 M:6:3 L:7 M:7:0 E:6 M:7:1
au:5 M:7:2 rc:5 M:7:3 L:8 M:8:0 E:7 M:8:1 au:6 M:8:2 rc:6 M:8:3 L:9 M:9:0 E:8 M:9:1 au:7 M:9:2 rc:7
M:9:3 L:10 M:10:0 E:9 M:10:1 au:8 M:10:2 rc:8 M:10:3 L:11 M:11:0 E:10 M:11:1 au:9 M:11:2 rc:9 M:11:3
L:12 M:12:0 E:11 M:12:1 au:10 M:12:2 rc:10 M:12:3 L:13 M:13:0 E:12 M:13:1 au:11 M:13:2 rc:11 M:13:3
L:14 M:14:0 E:13 M:14:1 au:12 M:14:2 rc:12 M:14:3 L:15 M:15:0 E:14 M:15:1 au:13 M:15:2 rc:13 M:15:3
E:15 au:14 rc:14 au:15 rc:15
"""


def carry(i):
    return (ROW * i) % 8


def down8(n):
    return n - n % 8


def up8(n):
    return n + (-n) % 8


def tile_adaptiveinputsoftmax_pa_kernel(tc, x, head_bytes, head_scale, tail_proj, tail_w, out_0, out_1):
    nc = tc.nc
    x_v = x.rearrange("a (q i) k -> (a q) i k", i=TILES)
    hb_v = head_bytes.rearrange("(g p t) n -> p g t n", p=P, t=4)
    sc_v = head_scale.rearrange("(g p t) o -> p g (t o)", p=P, t=4)
    pr_v = tail_proj.rearrange("(g p t) c -> p g (t c)", p=P, t=4)
    tw_v = tail_w.rearrange("(p t) n -> p t n", t=4)
    out_v = out_0.rearrange("a (q i) c -> (a q) (i c)", i=TILES)
    out1_v = out_1.rearrange("a (q i) o -> (a q) (i o)", i=TILES)

    with ExitStack() as ctx:
        keep = ctx.enter_context(tc.tile_pool(name="keep", bufs=1))
        work = ctx.enter_context(tc.tile_pool(name="work", bufs=1))
        psum = ctx.enter_context(tc.psum_pool(name="psum", bufs=8))

        ident32 = keep.tile([P, P], F32, name="ident32", align_bytes=64)
        ident16 = keep.tile([P, P], BF16, name="ident16", align_bytes=64)
        scale = keep.tile([P, 2, 4], F32, name="scale")
        xc = keep.tile([P, TILES, 256], U32, name="xc", align_bytes=64)
        xs = keep.tile([P, TILES, 256], U8, name="xs", align_bytes=64)
        hc = keep.tile([P, 2, HEAD], U32, name="hc", align_bytes=64)
        hs = keep.tile([P, 2, HEAD], U8, name="hs", align_bytes=64)
        pc = keep.tile([P, 2, H], U32, name="pc", align_bytes=64)
        ps = keep.tile([P, 2, H], U8, name="ps", align_bytes=64)
        yc = keep.tile([P, TILES, P], U32, name="yc", align_bytes=64)
        ys = keep.tile([P, TILES, P], U8, name="ys", align_bytes=64)
        wc = keep.tile([P, TAIL], U32, name="wc", align_bytes=64)
        ws = keep.tile([P, TAIL], U8, name="ws", align_bytes=64)
        other = keep.tile([P, TILES], F32, name="other")
        pair = keep.tile([P, TILES, 2], F32, name="pair")
        warm = keep.tile([P, 1], F32, name="warm")
        tail_raw = keep.tile([P, 4, TAIL], BF16, name="tail_raw", align_bytes=64)

        ctx.enter_context(tc.manual_schedule())

        early = {}
        late = {}
        raw = {}
        wide = {}
        grouped = {}
        xgrp = {}
        ygrp = {}
        rows = {}
        state = {}

        def load_all():
            nc.sync.dma_start(out=scale[:], in_=sc_v)
            hbytes, x_raw, proj_raw = raw["h"], raw["x"], raw["p"]

            def load_bytes(half, g, t0, t1):
                cols = slice(1024 * half, 1024 * (half + 1))
                nc.sync.dma_start(out=hbytes[:, g, t0:t1, cols], in_=hb_v[:, g, t0:t1, cols])

            def load_x(i):
                nc.sync.dma_start(out=x_raw[:, i:i + 2, :], in_=x_v[:, i:i + 2, :])

            for name in LOADS:
                if name[0] == "b":
                    half, g = int(name[1]), int(name[2])
                    t0, t1 = {"a": (0, 2), "b": (2, 4), "": (0, 4)}[name[3:]]
                    load_bytes(half, g, t0, t1)
                elif name[0] == "x":
                    load_x(2 * int(name[1]))
                elif name[0] == "p":
                    g = int(name[1])
                    nc.sync.dma_start(out=proj_raw[:, g, :], in_=pr_v[:, g, :])
                else:
                    cols = slice(1024 * int(name[1]), 1024 * (int(name[1]) + 1))
                    nc.sync.dma_start(out=tail_raw[:, :, cols], in_=tw_v[:, :, cols])

        def w(half, g):
            if g == 0:
                wide[half] = work.tile([P, 2, 4, 1024], BF16, name="wide", tag="row", bufs=4, align_bytes=64)
            for t in range(4):
                codes = raw["h"][:, g, t, 1024 * half:1024 * (half + 1)].bitcast(FP8)
                if (half, g, t) in WIDEN_S:
                    nc.scalar.activation(out=wide[half][:, g, t, :], in_=codes, func=COPY, scale=scale[:, g, t:t + 1])
                else:
                    nc.vector.tensor_scalar(
                        out=wide[half][:, g, t, :], in0=codes, scalar1=scale[:, g, t:t + 1], scalar2=None, op0=MULT,
                    )

        def x_(i):
            words = raw["x"][:, i, :].bitcast(F32)
            bank = psum.tile([P, 2, 2, P], F32, name="bank", tag="bank", bufs=8)
            for g in range(2):
                for u in range(2):
                    nc.tensor.transpose(bank[:, g, u, :], words[:, 256 * g + u:256 * (g + 1):2], ident32[:])
            if i // 2 not in xgrp:
                xgrp[i // 2] = early["pool"].tile([P, 2048], BF16, name="xgrp", tag="xgrp", bufs=XBUFS, align_bytes=64)
            copy = nc.vector.tensor_copy if i in X_V else nc.scalar.copy
            copy(
                out=xgrp[i // 2][:, 1024 * (i % 2):1024 * (i % 2 + 1)].bitcast(F32).rearrange("p (g r u) -> p g r u", g=2, u=2),
                in_=bank[:].rearrange("p g u r -> p g r u"),
            )

        def qx(k):
            nc.vector.quantize_mx(
                out=xc[:, 2 * k:2 * k + 2, :].rearrange("p i w -> p (i w)").bitcast(FP8X4),
                scales=xs[:, 2 * k:2 * k + 2, :].rearrange("p i w -> p (i w)"),
                in_=xgrp[k][:],
            )

        def u(kind, a, g=0):
            pool, bufs = (work, 4) if kind == "t" else (early["pool"], 2 if kind == "p" else HBUFS)
            out = pool.tile([P, 2048], BF16, name="grp_" + kind, tag="grp_" + kind, bufs=bufs, align_bytes=64)
            key = (kind, a, g) if kind == "h" else (kind, a)
            grouped[key] = out
            mode = UNITS[key]
            if kind == "p":
                src = raw["p"][:, a, :].rearrange("p (j m t) -> p t m j", j=4, t=4)
                dst = out[:].rearrange("p (t m j) -> p t m j", t=4, j=4)
                part = lambda k: src[:, k, :, :]
            else:
                if kind == "h":
                    n0 = BANK * (a % 2)
                    planes = wide[a // 2][:, g, :, n0:n0 + BANK]
                else:
                    planes = tail_raw[:, :, BANK * a:BANK * (a + 1)]
                src = planes.rearrange("p t (c i) -> p c t i", i=4)
                dst = out[:].rearrange("p (c i t) -> p c t i", i=4, t=4)
                part = lambda k: planes[:, :, 128 * k:128 * (k + 1)].rearrange("p t n -> p n t")
            if mode == "T":
                for b in range(2):
                    bank = psum.tile([P, 256, 4], BF16, name="bank", tag="bank", bufs=8)
                    for q in range(2):
                        nc.tensor.matmul(
                            out=bank[:, 128 * q:128 * (q + 1), :], lhsT=ident16[:], rhs=part(2 * b + q), start=True, stop=True,
                        )
                    nc.scalar.copy(
                        out=out[:, 1024 * b:1024 * (b + 1)].bitcast(F32),
                        in_=bank[:].rearrange("p n t -> p (n t)").bitcast(F32),
                    )
            elif mode == "G":
                nc.gpsimd.tensor_scalar(out=dst, in0=src, scalar1=1.0, scalar2=0.0, op0=MULT, op1=ADD)
            elif mode == "S":
                nc.scalar.copy(out=dst, in_=src)
            else:
                nc.vector.tensor_copy(out=dst, in_=src)

        def q(kind, a, g=0):
            if kind == "h":
                codes, scales, key = hc[:, g, a * BANK:(a + 1) * BANK], hs[:, g, a * BANK:(a + 1) * BANK], (kind, a, g)
            elif kind == "p":
                codes, scales, key = pc[:, a, :], ps[:, a, :], (kind, a)
            else:
                codes, scales, key = wc[:, BANK * a:BANK * (a + 1)], ws[:, BANK * a:BANK * (a + 1)], (kind, a)
            nc.vector.quantize_mx(out=codes.bitcast(FP8X4), scales=scales, in_=grouped[key][:])

        def y(k):
            ygrp[k] = work.tile([P, 2, P, 4], BF16, name="ygrp", tag="ygrp", bufs=4, align_bytes=64)
            for i in (2 * k, 2 * k + 1):
                bank = psum.tile([P, 4, P], F32, name="bank", tag="bank", bufs=8)
                for t in range(4):
                    for g in range(2):
                        nc.tensor.matmul_mx(
                            out=bank[:, t, :],
                            lhsT=pc[:, g, P * t:P * (t + 1)].bitcast(FP8X4),
                            lhsT_scale=ps[:, g, P * t:P * (t + 1)],
                            rhs=xc[:, i, P * g:P * (g + 1)].bitcast(FP8X4),
                            rhs_scale=xs[:, i, P * g:P * (g + 1)],
                            start=(g == 0),
                            stop=(g == 1),
                        )
                copy = nc.vector.tensor_copy if i in Y_V else nc.scalar.copy
                copy(out=ygrp[k][:, i % 2], in_=bank[:].rearrange("p t n -> p n t"))

        def qy(k):
            nc.vector.quantize_mx(
                out=yc[:, 2 * k:2 * k + 2, :].rearrange("p i n -> p (i n)").bitcast(FP8X4),
                scales=ys[:, 2 * k:2 * k + 2, :].rearrange("p i n -> p (i n)"),
                in_=ygrp[k][:].rearrange("p i n t -> p (i n t)"),
            )

        def L(n):
            kind, i = SEQ[n]
            banks = []
            for c in range(4):
                bank = psum.tile([P, BANK], F32, name="bank", tag="bank", bufs=8)
                cols = slice(BANK * c, BANK * (c + 1))
                if kind == "h":
                    for g in range(2):
                        nc.tensor.matmul_mx(
                            out=bank[:],
                            lhsT=xc[:, i, P * g:P * (g + 1)].bitcast(FP8X4),
                            lhsT_scale=xs[:, i, P * g:P * (g + 1)],
                            rhs=hc[:, g, cols].bitcast(FP8X4),
                            rhs_scale=hs[:, g, cols],
                            start=(g == 0),
                            stop=(g == 1),
                        )
                else:
                    nc.tensor.matmul_mx(
                        out=bank[:],
                        lhsT=yc[:, i, :].bitcast(FP8X4),
                        lhsT_scale=ys[:, i, :],
                        rhs=wc[:, cols].bitcast(FP8X4),
                        rhs_scale=ws[:, cols],
                        start=True,
                        stop=True,
                    )
                banks.append(bank)
            state[n] = {"banks": banks}

        def M(n, c):
            st = state[n]
            if c == 0:
                st["peaks"] = work.tile([P, 4], F32, name="peaks", tag="peaks", bufs=4)
            nc.vector.tensor_reduce(out=st["peaks"][:, c:c + 1], in_=st["banks"][c][:], axis=AX, op=MAX)

        def E(n):
            kind, i = SEQ[n]
            st = state[n]
            if kind == "h":
                if i >= 4:
                    rows[i] = late["pool"].tile([P, 4104], F32, name="late_row", tag="late_row", bufs=4, align_bytes=64)
                else:
                    rows[i] = work.tile([P, 4104], F32, name="row", tag="row", bufs=4, align_bytes=64)
            negmax = work.tile([P, 1], F32, name="negmax", tag="negmax", bufs=4)
            nc.vector.tensor_reduce(out=negmax[:], in_=st["peaks"][:], axis=AX, op=MAX, negate=True)
            st["sums"] = work.tile([P, 4], F32, name="sums4", tag="sums4", bufs=8)
            start = carry(i) + (0 if kind == "h" else TOKENS_OUT)
            for c in range(4):
                nc.scalar.activation(
                    out=rows[i][:, start + BANK * c:start + BANK * (c + 1)], in_=st["banks"][c][:], func=EXP,
                    bias=negmax[:], scale=1.0, accum_out=st["sums"][:, c:c + 1],
                )
            if kind == "h":
                st["clus"] = work.tile([P, 2], F32, name="clus", tag="clus", bufs=8)
                nc.scalar.copy(out=st["clus"][:], in_=rows[i][:, start + TOKENS_OUT:start + HEAD])

        def au(n):
            total = work.tile([P, 1], F32, name="total", tag="total", bufs=8)
            nc.vector.tensor_reduce(out=total[:], in_=state[n]["sums"][:], axis=AX, op=ADD)
            state[n]["total"] = total

        def rc(n):
            kind, i = SEQ[n]
            inv_t = work.tile([P, 1], F32, name="inv", tag="inv", bufs=8)
            inv = inv_t[:]
            nc.vector.reciprocal(out=inv, in_=state[n]["total"][:])
            row, c0 = rows[i], carry(i)
            split = down8(c0 + TOKENS_OUT)
            if SEQ[n] in ON_SCALAR:
                move = nc.scalar.copy

                def scaled(out, by):
                    if len(by) == 1:
                        nc.scalar.activation(out=out, in_=out, func=COPY, scale=by[0])
                    else:
                        both = work.tile([P, 1], F32, name="both", tag="both", bufs=4)
                        nc.scalar.activation(out=both[:], in_=by[0], func=COPY, scale=by[1])
                        nc.scalar.activation(out=out, in_=out, func=COPY, scale=both[:])
            else:
                engine = nc.vector if SEQ[n] in ON_VECTOR else nc.gpsimd
                move = engine.tensor_copy

                def scaled(out, by):
                    if len(by) == 1:
                        engine.tensor_scalar(out=out, in0=out, scalar1=by[0], scalar2=0.0, op0=MULT, op1=ADD)
                    else:
                        engine.tensor_scalar(out=out, in0=out, scalar1=by[0], scalar2=by[1], op0=MULT, op1=MULT)
            if kind == "h":
                if SEQ[n] in ON_SCALAR:
                    nc.scalar.activation(out=pair[:, i, :], in_=state[n]["clus"][:], func=COPY, scale=inv)
                else:
                    engine.tensor_scalar(out=pair[:, i, :], in0=state[n]["clus"][:], scalar1=inv, scalar2=0.0, op0=MULT, op1=ADD)
                scaled(row[:, c0:c0 + TOKENS_OUT], [inv])
                nc.sync.dma_start(out=out_v[:, ROW * i - c0 + up8(c0):ROW * i - c0 + split], in_=row[:, up8(c0):split])
                if i == TILES - 1:
                    nc.gpsimd.tensor_copy(out=other[:], in_=pair[:, :, 1])
                    nc.sync.dma_start(out=out1_v, in_=other[:])
            else:
                prob = pair[:, i, 0:1]
                base = c0 + TOKENS_OUT
                end = c0 + ROW
                if i < TILES - 1:
                    if up8(end) > end:
                        c1 = carry(i + 1)
                        move(out=row[:, end:up8(end)], in_=rows[i + 1][:, c1:8])
                    scaled(row[:, base:end], [inv, prob])
                    nc.sync.dma_start(out=out_v[:, ROW * i - c0 + split:ROW * i - c0 + up8(end)], in_=row[:, split:up8(end)])
                else:
                    for a in range(0, TAIL, 512):
                        scaled(row[:, base + a:base + a + 512], [inv, prob])
                        nc.sync.dma_start(out=out_v[:, ROW * i + TOKENS_OUT + a:ROW * i + TOKENS_OUT + a + 512], in_=row[:, base + a:base + a + 512])

        STEPS = {"w": w, "x": x_, "qx": qx, "u": u, "q": q, "y": y, "qy": qy, "L": L, "M": M, "E": E, "au": au, "rc": rc}

        def go(plan):
            for step in plan.split():
                parts = step.split(":")
                args = [int(a) if a not in "hpt" else a for a in parts[1:]]
                STEPS[parts[0]](*args)

        with tc.tile_pool(name="early", bufs=1) as early_pool:
            early["pool"] = early_pool
            raw_h = early_pool.tile([P, 2, 4, HEAD], U8, name="hbytes", align_bytes=64)
            raw_p = early_pool.tile([P, 2, 4 * H], BF16, name="proj_raw", align_bytes=64)
            raw_x = early_pool.tile([P, TILES, D_IN], BF16, name="x_raw", align_bytes=64)
            raw["h"], raw["p"], raw["x"] = raw_h, raw_p, raw_x
            load_all()
            nc.vector.memset(warm[:], 0.0)
            nc.scalar.activation(out=warm[:], in_=warm[:], func=EXP)
            make_identity(nc, ident32[:])
            make_identity(nc, ident16[:])
            go(PLAN_EARLY)
        late["pool"] = ctx.enter_context(tc.tile_pool(name="late", bufs=1))
        go(PLAN_LATE)
